import numpy as np
import ml_dtypes


def mxq(x, axis, fmt="e4m3"):
    dtype, down = {"e4m3": (ml_dtypes.float8_e4m3fn, 7), "e5m2": (ml_dtypes.float8_e5m2, 14)}[fmt]
    v = np.moveaxis(np.asarray(x, np.float32).astype(ml_dtypes.bfloat16).astype(np.float64), axis, -1)
    blocks = v.reshape(v.shape[:-1] + (-1, 32))
    amax = np.abs(blocks).max(-1, keepdims=True)
    byte = np.maximum(np.where(amax > 0, np.frexp(amax)[1] - 1 + 127, 0) - down, 1)
    scale = np.exp2(byte - 127.0)
    codes = (blocks / scale).astype(np.float32).astype(dtype).astype(np.float64)
    return np.moveaxis((codes * scale).reshape(v.shape), -1, axis)


WIDE = False


def mx_kscale(k):
    if not WIDE:
        return np.ones(k)
    levels = np.array([10, -10, 5, -5, 0])
    if k % 512:
        return np.exp2(np.random.permutation(np.resize(levels, k // 32))).repeat(32)
    a = np.empty((k // 512, 16))
    for p in range(k // 512):
        a[p, :8] = np.random.permutation(np.resize(levels, 8))
        for g in range(8):
            far = levels[np.abs(levels - a[p, g]) >= 10]
            a[p, g + 8] = far[np.random.randint(len(far))]
    return np.exp2(a.ravel()).repeat(32)


BF16 = ml_dtypes.bfloat16


def bf(x):
    return np.asarray(x, np.float32).astype(BF16)


def f64(x):
    return np.asarray(x).astype(np.float64)


B, N, DIM, H, D, M = 2, 3072, 2048, 32, 64, 16
HD = H * D


def sigmoid(v):
    return 1.0 / (1.0 + np.exp(-v))


def setup_inputs():
    s = mx_kscale(DIM)
    t = mx_kscale(HD)
    return {"attn_out": bf(np.random.standard_normal((B, H, N, D)) * 0.2 * t.reshape(H, 1, D)[None]),
            "hg_lin": bf(np.random.standard_normal((B, N, H))),
            "x": bf(np.random.standard_normal((B, N, DIM)) * s),
            "Wg": bf(np.random.standard_normal((DIM, HD)) / np.sqrt(DIM) / s[:, None]),
            "bg": bf(np.random.standard_normal(HD) * 0.3),
            "bhg": bf(np.random.standard_normal(H) * 0.3),
            "Wo": bf(np.random.standard_normal((HD, DIM)) * 3.0 / np.sqrt(HD) / t[:, None])}


def reference(attn_out, hg_lin, x, Wg, bg, bhg, Wo):
    head_gate = sigmoid(f64(hg_lin) + f64(bhg))
    o = f64(attn_out) * head_gate.transpose(0, 2, 1)[..., None]
    o = o.transpose(0, 2, 1, 3).reshape(B, N, HD)
    o = o * sigmoid((mxq(f64(x), 2, "e4m3") @ mxq(f64(Wg), 0, "e4m3")) + f64(bg))
    return mxq(o, 2, "e4m3") @ mxq(f64(Wo), 0, "e4m3")

@@ -1,0 +1,336 @@
+from contextlib import ExitStack
+
+import concourse.mybir as mybir
+from concourse.masks import make_identity
+
+B, N, DIM, H, D = 2, 3072, 2048, 32, 64
+HD = H * D
+FLOPS = 2 * B * N * DIM * HD + 2 * B * N * HD * DIM
+
+F32 = mybir.dt.float32
+BF16 = mybir.dt.bfloat16
+U32 = mybir.dt.uint32
+U8 = mybir.dt.uint8
+FP8X4 = mybir.dt.float8_e4m3fn_x4
+MULT = mybir.AluOpType.mult
+ADD = mybir.AluOpType.add
+SIGMOID = mybir.ActivationFunctionType.Sigmoid
+
+P = 128
+BLK = 512
+NBLK = B * N // BLK
+BLK_PER_B = N // BLK
+NSTEP = 4 * NBLK
+LAG = 4
+RAW_BUFS = 6
+
+
+def tile_attention_pb_l_kernel(tc, attn_out, hg_lin, x, Wg, bg, bhg, Wo, out):
+    nc = tc.nc
+
+    x_v = x.rearrange("b (i p j) k -> b i p j k", p=P, j=4)
+    a_v = attn_out.rearrange("b h (i p j) d -> b i p h (j d)", p=P, j=4)
+    hg_v = hg_lin.rearrange("b (i p j) h -> p (b i) (j h)", p=P, j=4)
+    out_v = out.rearrange("b (i r j) c -> b i j r c", r=P, j=4)
+    wg_v = Wg.rearrange("(g p j) c -> g p j c", p=P, j=4)
+    wo_v = Wo.rearrange("(g p j) c -> g p j c", p=P, j=4)
+    bg_v = bg.rearrange("(g p t) -> p g t", p=P, t=4)
+
+    with ExitStack() as ctx:
+        keep = ctx.enter_context(tc.tile_pool(name="keep", bufs=1))
+        sb = ctx.enter_context(tc.tile_pool(name="sb", bufs=2))
+        ps = ctx.enter_context(tc.psum_pool(name="ps", bufs=4))
+        ctx.enter_context(tc.manual_schedule())
+
+        ident = keep.tile([P, P], F32, name="ident")
+        wgq = keep.tile([P, 4, HD], U32, name="wgq", align_bytes=64)
+        wgs = keep.tile([P, 4, HD], U8, name="wgs", align_bytes=64)
+        woq = keep.tile([P, 4, DIM], U32, name="woq", align_bytes=64)
+        wos = keep.tile([P, 4, DIM], U8, name="wos", align_bytes=64)
+        hgs = keep.tile([P, 4 * NBLK, H], F32, name="hgs")
+        bh = keep.tile([P, H], BF16, name="bh")
+        bgb = keep.tile([P, 4, 4], BF16, name="bgb")
+        bgt = keep.tile([P, 16], F32, name="bgt")
+        warm = keep.tile([P, 1], F32, name="warm")
+        warm2 = keep.tile([P, 1], F32, name="warm2")
+
+        order = []
+        for c in range(4):
+            order.extend([("wg", c, g) for g in range(4)])
+            order.append(("a", c, 0))
+        for c in range(4):
+            order.extend([("wo", c, g) for g in range(4)])
+            order.append(("a", 4 + c, 0))
+        order.extend([("a", n, 0) for n in range(8, NSTEP)])
+
+        raw = {}
+        xraw = {}
+        xq = {}
+        yq = {}
+        gated = {}
+        state = {"next": 0, "used": 0, "xnext": 0, "xused": 0, "pending": []}
+
+        def fetch():
+            lo = state["next"]
+            hi = min(len(order), state["used"] + RAW_BUFS)
+            for q in range(lo, hi):
+                kind, c, g = order[q]
+                t = sb.tile([P, 2048], BF16, name="raw", tag="raw", bufs=RAW_BUFS)
+                if kind == "a":
+                    blk, grp = divmod(c, 4)
+                    b, i = divmod(blk, BLK_PER_B)
+                    nc.sync.dma_start(
+                        out=t[:].rearrange("p (h e) -> p h e", h=8),
+                        in_=a_v[b, i][:, 8 * grp : 8 * grp + 8, :],
+                    )
+                else:
+                    src = wg_v if kind == "wg" else wo_v
+                    nc.sync.dma_start(
+                        out=t[:].rearrange("p (j c) -> p j c", j=4),
+                        in_=src[g][:, :, 512 * c : 512 * (c + 1)],
+                    )
+                raw[(kind, c, g)] = t
+            state["next"] = max(lo, hi)
+
+        def fetch_x():
+            m = state["xnext"]
+            if m < 2 * NBLK and m < state["xused"] + 2:
+                blk, h = divmod(m, 2)
+                b, i = divmod(blk, BLK_PER_B)
+                t = sb.tile([P, 4, 1024], BF16, name="xr", tag="xr", bufs=2)
+                nc.sync.dma_start(out=t[:], in_=x_v[b, i][:, :, 1024 * h : 1024 * (h + 1)])
+                xraw[m] = t
+                state["xnext"] = m + 1
+
+        def transpose_x(m):
+            blk, h = divmod(m, 2)
+            xr = xraw[m]
+            for gl in range(2):
+                xg = sb.tile([P, 2048], BF16, name="xg", tag="grp", bufs=4, align_bytes=64)
+                xgw = xg[:].bitcast(F32).rearrange("p (n u) -> p n u", u=2)
+                for jp in range(2):
+                    bank = ps.tile([P, 2, 2, P], F32, name="xt", tag="tp", bufs=4)
+                    for jj in range(2):
+                        words = xr[:, 2 * jp + jj, :].bitcast(F32)
+                        for u in range(2):
+                            nc.tensor.transpose(
+                                bank[:, jj, u, :],
+                                words[:, 256 * gl + u : 256 * (gl + 1) : 2],
+                                ident[:],
+                            )
+                    nc.scalar.copy(
+                        out=xgw[:, 256 * jp : 256 * (jp + 1), :].rearrange(
+                            "p (jj r) u -> p jj r u", jj=2
+                        ),
+                        in_=bank[:].rearrange("p jj u r -> p jj r u"),
+                    )
+                state["pending"].append((blk, 2 * h + gl, xg))
+            state["xused"] = m + 1
+
+        def quantize_x():
+            for blk, g, xg in state["pending"]:
+                if g == 0:
+                    codes = sb.tile([P, 4, BLK], U32, name="xq", tag="xq", bufs=2, align_bytes=64)
+                    scales = sb.tile([P, 4, BLK], U8, name="xs", tag="xs", bufs=2, align_bytes=64)
+                    xq[blk] = (codes, scales)
+                codes, scales = xq[blk]
+                nc.vector.quantize_mx(
+                    out=codes[:, g, :].bitcast(FP8X4), scales=scales[:, g, :], in_=xg[:]
+                )
+            state["pending"] = []
+
+        def group_w(copy, kind, c, g):
+            wr = raw[(kind, c, g)]
+            wgp = sb.tile([P, 2048], BF16, name="wgp", tag="grp", bufs=4, align_bytes=64)
+            if kind == "wg":
+                copy(
+                    out=wgp[:].rearrange("p (t m j) -> p t m j", t=4, j=4),
+                    in_=wr[:].rearrange("p (j m t) -> p t m j", j=4, t=4),
+                )
+            else:
+                copy(
+                    out=wgp[:].rearrange("p (n j) -> p n j", j=4),
+                    in_=wr[:].rearrange("p (j n) -> p n j", j=4),
+                )
+            state["used"] = state["used"] + 1
+            return wgp
+
+        def quantize_w(kind, c, g, wgp):
+            codes, scales = (wgq, wgs) if kind == "wg" else (woq, wos)
+            cols = slice(512 * c, 512 * (c + 1))
+            nc.vector.quantize_mx(
+                out=codes[:, g, cols].bitcast(FP8X4), scales=scales[:, g, cols], in_=wgp[:]
+            )
+
+        def gate_heads(n, j):
+            blk, grp = divmod(n, 4)
+            ar = raw[("a", n, 0)][:].rearrange("p (h e) -> p h e", h=8)
+            ah = sb.tile([P, 512], F32, name="ah", tag="ah", bufs=8)
+            nc.vector.tensor_tensor(
+                out=ah[:].rearrange("p (t h m) -> p t h m", t=4, h=8),
+                in0=ar[:, :, 64 * j : 64 * (j + 1)].rearrange("p h (m t) -> p t h m", t=4),
+                in1=hgs[:, 4 * blk + j, 8 * grp : 8 * grp + 8]
+                .unsqueeze(1)
+                .unsqueeze(3)
+                .to_broadcast([P, 4, 8, 16]),
+                op=MULT,
+            )
+            gated[(n, j)] = ah
+            if j == 3:
+                state["used"] = state["used"] + 1
+
+        def stage1(n, extra):
+            blk, grp = divmod(n, 4)
+            codes, scales = xq[blk]
+            gt = sb.tile([P, 4, BLK], F32, name="gt", tag="g", bufs=2)
+            grouped = []
+            for t in range(4):
+                acc = ps.tile([P, BLK], F32, name="acc", tag="acc", bufs=4)
+                cols = slice(512 * grp + P * t, 512 * grp + P * (t + 1))
+                for g in range(4):
+                    nc.tensor.matmul_mx(
+                        out=acc[:],
+                        lhsT=wgq[:, g, cols].bitcast(FP8X4),
+                        lhsT_scale=wgs[:, g, cols],
+                        rhs=codes[:, g, :].bitcast(FP8X4),
+                        rhs_scale=scales[:, g, :],
+                        start=(g == 0),
+                        stop=(g == 3),
+                    )
+                nc.scalar.activation(
+                    out=gt[:, t, :],
+                    in_=acc[:],
+                    func=SIGMOID,
+                    bias=bgt[:, 4 * grp + t : 4 * grp + t + 1],
+                    scale=1.0,
+                )
+                if t < len(extra):
+                    kind, c, g = extra[t]
+                    grouped.append(group_w(nc.scalar.copy, kind, c, g))
+            return gt, grouped
+
+        def gate_features(n, gt):
+            blk, grp = divmod(n, 4)
+            banks = []
+            for j in range(4):
+                bank = ps.tile([P, 4, P], F32, name="at", tag="tp", bufs=4)
+                ah = gated[(n, j)]
+                for t in range(4):
+                    nc.tensor.transpose(bank[:, t, :], ah[:, P * t : P * (t + 1)], ident[:])
+                banks.append(bank)
+            yg = sb.tile([P, BLK, 4], BF16, name="yg", tag="yg", bufs=2, align_bytes=64)
+            for j in range(4):
+                nc.vector.tensor_tensor(
+                    out=yg[:, P * j : P * (j + 1), :],
+                    in0=gt[:, :, P * j : P * (j + 1)].rearrange("p t r -> p r t"),
+                    in1=banks[j][:].rearrange("p t r -> p r t"),
+                    op=MULT,
+                )
+            return yg
+
+        def quantize_y(n, yg):
+            blk, grp = divmod(n, 4)
+            if grp == 0:
+                codes = sb.tile([P, 4, BLK], U32, name="yq", tag="yq", bufs=2, align_bytes=64)
+                scales = sb.tile([P, 4, BLK], U8, name="ys", tag="ys", bufs=2, align_bytes=64)
+                yq[blk] = (codes, scales)
+            codes, scales = yq[blk]
+            nc.vector.quantize_mx(
+                out=codes[:, grp, :].bitcast(FP8X4),
+                scales=scales[:, grp, :],
+                in_=yg[:].rearrange("p n t -> p (n t)"),
+            )
+
+        def stage2(m):
+            blk, oc = divmod(m, 4)
+            b, i = divmod(blk, BLK_PER_B)
+            codes, scales = yq[blk]
+            cols = slice(512 * oc, 512 * (oc + 1))
+            for j in range(4):
+                acc = ps.tile([P, 512], F32, name="acc", tag="acc", bufs=4)
+                toks = slice(P * j, P * (j + 1))
+                for g in range(4):
+                    nc.tensor.matmul_mx(
+                        out=acc[:],
+                        lhsT=codes[:, g, toks].bitcast(FP8X4),
+                        lhsT_scale=scales[:, g, toks],
+                        rhs=woq[:, g, cols].bitcast(FP8X4),
+                        rhs_scale=wos[:, g, cols],
+                        start=(g == 0),
+                        stop=(g == 3),
+                    )
+                ot = sb.tile([P, 512], F32, name="ot", tag="o", bufs=4)
+                nc.scalar.copy(out=ot[:], in_=acc[:])
+                nc.sync.dma_start(out=out_v[b, i, j][:, cols], in_=ot[:])
+
+        hl = sb.tile([P, NBLK, 4 * H], BF16, name="hl", tag="g", bufs=2)
+        nc.scalar.dma_start(out=hl[:], in_=hg_v)
+        nc.scalar.dma_start(out=bh[:], in_=bhg.partition_broadcast(P))
+        nc.scalar.dma_start(out=bgb[:], in_=bg_v)
+        fetch_x()
+        fetch_x()
+        fetch()
+        make_identity(nc, ident[:])
+        nc.vector.memset(warm[:], 0.0)
+        nc.scalar.activation(out=warm2[:], in_=warm[:], func=SIGMOID)
+        nc.vector.tensor_copy(out=bgt[:], in_=bgb[:].rearrange("p g t -> p (g t)"))
+        nc.vector.tensor_tensor(
+            out=hgs[:],
+            in0=hl[:].rearrange("p a (j h) -> p (a j) h", j=4),
+            in1=bh[:].unsqueeze(1).to_broadcast([P, 4 * NBLK, H]),
+            op=ADD,
+        )
+        nc.scalar.activation(out=hgs[:], in_=hgs[:], func=SIGMOID)
+        transpose_x(0)
+        quantize_x()
+        transpose_x(1)
+        w0 = group_w(nc.vector.tensor_copy, "wg", 0, 0)
+        quantize_x()
+        w1 = group_w(nc.vector.tensor_copy, "wg", 0, 1)
+        w2 = group_w(nc.scalar.copy, "wg", 0, 2)
+        w3 = group_w(nc.scalar.copy, "wg", 0, 3)
+        quantize_w("wg", 0, 0, w0)
+        quantize_w("wg", 0, 1, w1)
+        quantize_w("wg", 0, 2, w2)
+        quantize_w("wg", 0, 3, w3)
+        for j in range(4):
+            gate_heads(0, j)
+
+        for s in range(NSTEP + LAG):
+            fetch()
+            fetch_x()
+            quantize_x()
+            chunk = None
+            if s < 3:
+                chunk = ("wg", s + 1)
+            elif s < 7:
+                chunk = ("wo", s - 3)
+            extra = []
+            if chunk is not None:
+                kind, c = chunk
+                w0 = group_w(nc.vector.tensor_copy, kind, c, 0)
+                w1 = group_w(nc.vector.tensor_copy, kind, c, 1)
+                extra = [(kind, c, 2), (kind, c, 3)]
+            if s + 1 < NSTEP:
+                gate_heads(s + 1, 0)
+            if chunk is not None:
+                quantize_w(kind, c, 0, w0)
+            if s + 1 < NSTEP:
+                gate_heads(s + 1, 1)
+            if chunk is not None:
+                quantize_w(kind, c, 1, w1)
+            if s + 1 < NSTEP:
+                gate_heads(s + 1, 2)
+                gate_heads(s + 1, 3)
+            if s < NSTEP:
+                gt, late = stage1(s, extra)
+                if chunk is not None:
+                    quantize_w(kind, c, 2, late[0])
+                    quantize_w(kind, c, 3, late[1])
+                yg = gate_features(s, gt)
+            if s >= LAG:
+                stage2(s - LAG)
+            if s < NSTEP:
+                quantize_y(s, yg)
+            if s % 2 == 0 and s // 2 + 2 < 2 * NBLK:
+                transpose_x(s // 2 + 2)

@@ -23,6 +23,8 @@ BLK_PER_B = N // BLK
 NSTEP = 4 * NBLK
 LAG = 4
 RAW_BUFS = 6
+NV = [2, 2, 2, 2, 2, 2, 2]
+SORT_FROM = 6
 
 
 def tile_attention_pb_l_kernel(tc, attn_out, hg_lin, x, Wg, bg, bhg, Wo, out):
@@ -54,17 +56,17 @@ def tile_attention_pb_l_kernel(tc, attn_out, hg_lin, x, Wg, bg, bhg, Wo, out):
         warm = keep.tile([P, 1], F32, name="warm")
         warm2 = keep.tile([P, 1], F32, name="warm2")
 
-        order = []
-        for c in range(4):
-            order.extend([("wg", c, g) for g in range(4)])
-            order.append(("a", c, 0))
-        for c in range(4):
-            order.extend([("wo", c, g) for g in range(4)])
-            order.append(("a", 4 + c, 0))
+        order = [("wg", 0, g) for g in range(4)] + [("a", 0, 0)]
+        for q in range(7):
+            kind, c = ("wg", q + 1) if q < 3 else ("wo", q - 3)
+            order.extend([(kind, c, g) for g in range(NV[q])])
+            order.append(("a", q + 1, 0))
+            order.extend([(kind, c, g) for g in range(NV[q], 4)])
         order.extend([("a", n, 0) for n in range(8, NSTEP)])
 
         raw = {}
         xraw = {}
+        xsorted = {}
         xq = {}
         yq = {}
         gated = {}
@@ -102,22 +104,34 @@ def tile_attention_pb_l_kernel(tc, attn_out, hg_lin, x, Wg, bg, bhg, Wo, out):
                 xraw[m] = t
                 state["xnext"] = m + 1
 
+        def sort_x(m):
+            if m < SORT_FROM:
+                return
+            words = xraw[m][:].rearrange("p j k -> p (j k)").bitcast(F32)
+            xo = sb.tile([P, 4, 2, 2, P], F32, name="xo", tag="xo", bufs=1)
+            for gl in range(2):
+                nc.vector.tensor_copy(
+                    out=xo[:, :, gl, :, :],
+                    in_=words.rearrange("p (j g w u) -> p j g u w", j=4, g=2, u=2)[:, :, gl, :, :],
+                )
+            xsorted[m] = xo
+            state["xused"] = m + 1
+
         def transpose_x(m):
             blk, h = divmod(m, 2)
-            xr = xraw[m]
             for gl in range(2):
                 xg = sb.tile([P, 2048], BF16, name="xg", tag="grp", bufs=4, align_bytes=64)
                 xgw = xg[:].bitcast(F32).rearrange("p (n u) -> p n u", u=2)
                 for jp in range(2):
                     bank = ps.tile([P, 2, 2, P], F32, name="xt", tag="tp", bufs=4)
                     for jj in range(2):
-                        words = xr[:, 2 * jp + jj, :].bitcast(F32)
                         for u in range(2):
-                            nc.tensor.transpose(
-                                bank[:, jj, u, :],
-                                words[:, 256 * gl + u : 256 * (gl + 1) : 2],
-                                ident[:],
-                            )
+                            if m < SORT_FROM:
+                                words = xraw[m][:, 2 * jp + jj, :].bitcast(F32)
+                                piece = words[:, 256 * gl + u : 256 * (gl + 1) : 2]
+                            else:
+                                piece = xsorted[m][:, 2 * jp + jj, gl, u, :]
+                            nc.tensor.transpose(bank[:, jj, u, :], piece, ident[:])
                     nc.scalar.copy(
                         out=xgw[:, 256 * jp : 256 * (jp + 1), :].rearrange(
                             "p (jj r) u -> p jj r u", jj=2
@@ -125,7 +139,8 @@ def tile_attention_pb_l_kernel(tc, attn_out, hg_lin, x, Wg, bg, bhg, Wo, out):
                         in_=bank[:].rearrange("p jj u r -> p jj r u"),
                     )
                 state["pending"].append((blk, 2 * h + gl, xg))
-            state["xused"] = m + 1
+            if m < SORT_FROM:
+                state["xused"] = m + 1
 
         def quantize_x():
             for blk, g, xg in state["pending"]:
@@ -263,7 +278,7 @@ def tile_attention_pb_l_kernel(tc, attn_out, hg_lin, x, Wg, bg, bhg, Wo, out):
                 nc.scalar.copy(out=ot[:], in_=acc[:])
                 nc.sync.dma_start(out=out_v[b, i, j][:, cols], in_=ot[:])
 
-        hl = sb.tile([P, NBLK, 4 * H], BF16, name="hl", tag="g", bufs=2)
+        hl = sb.tile([P, NBLK, 4 * H], BF16, name="hl", tag="xo", bufs=1)
         nc.scalar.dma_start(out=hl[:], in_=hg_v)
         nc.scalar.dma_start(out=bh[:], in_=bhg.partition_broadcast(P))
         nc.scalar.dma_start(out=bgb[:], in_=bg_v)
@@ -274,15 +289,21 @@ def tile_attention_pb_l_kernel(tc, attn_out, hg_lin, x, Wg, bg, bhg, Wo, out):
         nc.vector.memset(warm[:], 0.0)
         nc.scalar.activation(out=warm2[:], in_=warm[:], func=SIGMOID)
         nc.vector.tensor_copy(out=bgt[:], in_=bgb[:].rearrange("p g t -> p (g t)"))
-        nc.vector.tensor_tensor(
-            out=hgs[:],
-            in0=hl[:].rearrange("p a (j h) -> p (a j) h", j=4),
-            in1=bh[:].unsqueeze(1).to_broadcast([P, 4 * NBLK, H]),
-            op=ADD,
-        )
-        nc.scalar.activation(out=hgs[:], in_=hgs[:], func=SIGMOID)
+
+        def head_gates(lo, hi):
+            nc.vector.tensor_tensor(
+                out=hgs[:, lo:hi, :],
+                in0=hl[:].rearrange("p a (j h) -> p (a j) h", j=4)[:, lo:hi, :],
+                in1=bh[:].unsqueeze(1).to_broadcast([P, hi - lo, H]),
+                op=ADD,
+            )
+            nc.scalar.activation(out=hgs[:, lo:hi, :], in_=hgs[:, lo:hi, :], func=SIGMOID)
+
+        head_gates(0, 12)
+        sort_x(0)
         transpose_x(0)
         quantize_x()
+        sort_x(1)
         transpose_x(1)
         w0 = group_w(nc.vector.tensor_copy, "wg", 0, 0)
         quantize_x()
@@ -295,38 +316,40 @@ def tile_attention_pb_l_kernel(tc, attn_out, hg_lin, x, Wg, bg, bhg, Wo, out):
         quantize_w("wg", 0, 3, w3)
         for j in range(4):
             gate_heads(0, j)
+        fetch_x()
+        sort_x(2)
 
         for s in range(NSTEP + LAG):
             fetch()
             fetch_x()
             quantize_x()
+            if s == 5:
+                head_gates(12, 4 * NBLK)
+            if s % 2 == 1 and (s + 5) // 2 < 2 * NBLK:
+                sort_x((s + 5) // 2)
             chunk = None
             if s < 3:
                 chunk = ("wg", s + 1)
             elif s < 7:
                 chunk = ("wo", s - 3)
             extra = []
+            early = []
             if chunk is not None:
                 kind, c = chunk
-                w0 = group_w(nc.vector.tensor_copy, kind, c, 0)
-                w1 = group_w(nc.vector.tensor_copy, kind, c, 1)
-                extra = [(kind, c, 2), (kind, c, 3)]
-            if s + 1 < NSTEP:
-                gate_heads(s + 1, 0)
-            if chunk is not None:
-                quantize_w(kind, c, 0, w0)
-            if s + 1 < NSTEP:
-                gate_heads(s + 1, 1)
-            if chunk is not None:
-                quantize_w(kind, c, 1, w1)
-            if s + 1 < NSTEP:
-                gate_heads(s + 1, 2)
-                gate_heads(s + 1, 3)
+                nv = NV[s]
+                early = [group_w(nc.vector.tensor_copy, kind, c, g) for g in range(nv)]
+                extra = [(kind, c, g) for g in range(nv, 4)]
+            for j in range(4):
+                if s + 1 < NSTEP:
+                    gate_heads(s + 1, j)
+                if j < len(early):
+                    quantize_w(kind, c, j, early[j])
+            fetch()
             if s < NSTEP:
                 gt, late = stage1(s, extra)
-                if chunk is not None:
-                    quantize_w(kind, c, 2, late[0])
-                    quantize_w(kind, c, 3, late[1])
+                fetch()
+                for q in range(len(late)):
+                    quantize_w(kind, c, len(early) + q, late[q])
                 yg = gate_features(s, gt)
             if s >= LAG:
                 stage2(s - LAG)

@@ -24,7 +24,9 @@ NSTEP = 4 * NBLK
 LAG = 4
 RAW_BUFS = 6
 NV = [2, 2, 2, 2, 2, 2, 2]
-SORT_FROM = 6
+SORT_FROM = 12
+TP_BUFS = 5
+ACC_BUFS = 3
 
 
 def tile_attention_pb_l_kernel(tc, attn_out, hg_lin, x, Wg, bg, bhg, Wo, out):
@@ -69,7 +71,9 @@ def tile_attention_pb_l_kernel(tc, attn_out, hg_lin, x, Wg, bg, bhg, Wo, out):
         xsorted = {}
         xq = {}
         yq = {}
-        gated = {}
+        asorted = {}
+        spread = {}
+        gateT = {}
         state = {"next": 0, "used": 0, "xnext": 0, "xused": 0, "pending": []}
 
         def fetch():
@@ -104,46 +108,49 @@ def tile_attention_pb_l_kernel(tc, attn_out, hg_lin, x, Wg, bg, bhg, Wo, out):
                 xraw[m] = t
                 state["xnext"] = m + 1
 
-        def sort_x(m):
-            if m < SORT_FROM:
+        def sort_x(q):
+            if q < SORT_FROM or q >= NSTEP:
                 return
+            m, gl = divmod(q, 2)
             words = xraw[m][:].rearrange("p j k -> p (j k)").bitcast(F32)
-            xo = sb.tile([P, 4, 2, 2, P], F32, name="xo", tag="xo", bufs=1)
-            for gl in range(2):
-                nc.vector.tensor_copy(
-                    out=xo[:, :, gl, :, :],
-                    in_=words.rearrange("p (j g w u) -> p j g u w", j=4, g=2, u=2)[:, :, gl, :, :],
-                )
-            xsorted[m] = xo
-            state["xused"] = m + 1
+            xo = sb.tile([P, 4, 2, P], F32, name="xo", tag="xo", bufs=2)
+            nc.vector.tensor_copy(
+                out=xo[:],
+                in_=words.rearrange("p (j g w u) -> p j g u w", j=4, g=2, u=2)[:, :, gl, :, :],
+            )
+            xsorted[q] = xo
+            if gl == 1:
+                state["xused"] = m + 1
 
-        def transpose_x(m):
-            blk, h = divmod(m, 2)
-            for gl in range(2):
-                xg = sb.tile([P, 2048], BF16, name="xg", tag="grp", bufs=4, align_bytes=64)
-                xgw = xg[:].bitcast(F32).rearrange("p (n u) -> p n u", u=2)
-                for jp in range(2):
-                    bank = ps.tile([P, 2, 2, P], F32, name="xt", tag="tp", bufs=4)
-                    for jj in range(2):
-                        for u in range(2):
-                            if m < SORT_FROM:
-                                words = xraw[m][:, 2 * jp + jj, :].bitcast(F32)
-                                piece = words[:, 256 * gl + u : 256 * (gl + 1) : 2]
-                            else:
-                                piece = xsorted[m][:, 2 * jp + jj, gl, u, :]
-                            nc.tensor.transpose(bank[:, jj, u, :], piece, ident[:])
-                    nc.scalar.copy(
-                        out=xgw[:, 256 * jp : 256 * (jp + 1), :].rearrange(
-                            "p (jj r) u -> p jj r u", jj=2
-                        ),
-                        in_=bank[:].rearrange("p jj u r -> p jj r u"),
-                    )
-                state["pending"].append((blk, 2 * h + gl, xg))
-            if m < SORT_FROM:
+        def transpose_x(q):
+            if q >= NSTEP:
+                return
+            m, gl = divmod(q, 2)
+            xg = sb.tile([P, 2048], BF16, name="xg", tag="grp", bufs=4, align_bytes=64)
+            xgw = xg[:].bitcast(F32).rearrange("p (n u) -> p n u", u=2)
+            for jp in range(2):
+                bank = ps.tile([P, 2, 2, P], F32, name="xt", tag="tp", bufs=TP_BUFS)
+                for jj in range(2):
+                    for u in range(2):
+                        if q < SORT_FROM:
+                            words = xraw[m][:, 2 * jp + jj, :].bitcast(F32)
+                            piece = words[:, 256 * gl + u : 256 * (gl + 1) : 2]
+                        else:
+                            piece = xsorted[q][:, 2 * jp + jj, u, :]
+                        nc.tensor.transpose(bank[:, jj, u, :], piece, ident[:])
+                nc.scalar.copy(
+                    out=xgw[:, 256 * jp : 256 * (jp + 1), :].rearrange(
+                        "p (jj r) u -> p jj r u", jj=2
+                    ),
+                    in_=bank[:].rearrange("p jj u r -> p jj r u"),
+                )
+            state["pending"].append((q, xg))
+            if q < SORT_FROM and gl == 1:
                 state["xused"] = m + 1
 
         def quantize_x():
-            for blk, g, xg in state["pending"]:
+            for q, xg in state["pending"]:
+                blk, g = divmod(q, 4)
                 if g == 0:
                     codes = sb.tile([P, 4, BLK], U32, name="xq", tag="xq", bufs=2, align_bytes=64)
                     scales = sb.tile([P, 4, BLK], U8, name="xs", tag="xs", bufs=2, align_bytes=64)
@@ -177,22 +184,51 @@ def tile_attention_pb_l_kernel(tc, attn_out, hg_lin, x, Wg, bg, bhg, Wo, out):
                 out=codes[:, g, cols].bitcast(FP8X4), scales=scales[:, g, cols], in_=wgp[:]
             )
 
-        def gate_heads(n, j):
-            blk, grp = divmod(n, 4)
-            ar = raw[("a", n, 0)][:].rearrange("p (h e) -> p h e", h=8)
-            ah = sb.tile([P, 512], F32, name="ah", tag="ah", bufs=8)
+        def head_gates(lo, hi):
             nc.vector.tensor_tensor(
-                out=ah[:].rearrange("p (t h m) -> p t h m", t=4, h=8),
-                in0=ar[:, :, 64 * j : 64 * (j + 1)].rearrange("p h (m t) -> p t h m", t=4),
-                in1=hgs[:, 4 * blk + j, 8 * grp : 8 * grp + 8]
-                .unsqueeze(1)
+                out=hgs[:, lo:hi, :],
+                in0=hl[:].rearrange("p a (j h) -> p (a j) h", j=4)[:, lo:hi, :],
+                in1=bh[:].unsqueeze(1).to_broadcast([P, hi - lo, H]),
+                op=ADD,
+            )
+            nc.scalar.activation(out=hgs[:, lo:hi, :], in_=hgs[:, lo:hi, :], func=SIGMOID)
+
+        def sort_a(n):
+            if n >= NSTEP:
+                return
+            words = raw[("a", n, 0)][:].bitcast(F32).rearrange(
+                "p (h j m u) -> p u j h m", h=8, j=4, u=2
+            )
+            ao = sb.tile([P, 4, 2, P], F32, name="ao", tag="ao", bufs=2)
+            for u in range(2):
+                nc.vector.tensor_copy(
+                    out=ao[:, :, u, :].rearrange("p j (h m) -> p j h m", h=8), in_=words[:, u]
+                )
+            asorted[n] = ao
+            state["used"] = state["used"] + 1
+
+        def spread_gates(n):
+            if n >= NSTEP:
+                return
+            blk, grp = divmod(n, 4)
+            sp = sb.tile([P, 4, P], F32, name="sp", tag="sp", bufs=2)
+            nc.vector.tensor_copy(
+                out=sp[:].rearrange("p j (h r) -> p j h r", h=8),
+                in_=hgs[:, 4 * blk : 4 * blk + 4, 8 * grp : 8 * grp + 8]
                 .unsqueeze(3)
                 .to_broadcast([P, 4, 8, 16]),
-                op=MULT,
             )
-            gated[(n, j)] = ah
-            if j == 3:
-                state["used"] = state["used"] + 1
+            spread[n] = sp
+
+        def transpose_gates(n):
+            if n >= NSTEP:
+                return
+            bank = ps.tile([P, 4, P], F32, name="ht", tag="tp", bufs=TP_BUFS)
+            for j in range(4):
+                nc.tensor.transpose(bank[:, j, :], spread[n][:, j, :], ident[:])
+            hgT = sb.tile([P, BLK], F32, name="hgT", tag="hgT", bufs=2)
+            nc.scalar.copy(out=hgT[:], in_=bank[:].rearrange("p j r -> p (j r)"))
+            gateT[n] = hgT
 
         def stage1(n, extra):
             blk, grp = divmod(n, 4)
@@ -200,7 +236,7 @@ def tile_attention_pb_l_kernel(tc, attn_out, hg_lin, x, Wg, bg, bhg, Wo, out):
             gt = sb.tile([P, 4, BLK], F32, name="gt", tag="g", bufs=2)
             grouped = []
             for t in range(4):
-                acc = ps.tile([P, BLK], F32, name="acc", tag="acc", bufs=4)
+                acc = ps.tile([P, BLK], F32, name="acc", tag="acc", bufs=ACC_BUFS)
                 cols = slice(512 * grp + P * t, 512 * grp + P * (t + 1))
                 for g in range(4):
                     nc.tensor.matmul_mx(
@@ -219,26 +255,34 @@ def tile_attention_pb_l_kernel(tc, attn_out, hg_lin, x, Wg, bg, bhg, Wo, out):
                     bias=bgt[:, 4 * grp + t : 4 * grp + t + 1],
                     scale=1.0,
                 )
+                nc.vector.tensor_tensor(
+                    out=gt[:, t, :], in0=gt[:, t, :], in1=gateT[n][:], op=MULT
+                )
                 if t < len(extra):
                     kind, c, g = extra[t]
                     grouped.append(group_w(nc.scalar.copy, kind, c, g))
             return gt, grouped
 
-        def gate_features(n, gt):
-            blk, grp = divmod(n, 4)
+        def transpose_a(n):
             banks = []
-            for j in range(4):
-                bank = ps.tile([P, 4, P], F32, name="at", tag="tp", bufs=4)
-                ah = gated[(n, j)]
-                for t in range(4):
-                    nc.tensor.transpose(bank[:, t, :], ah[:, P * t : P * (t + 1)], ident[:])
+            for jp in range(2):
+                bank = ps.tile([P, 2, 2, P], F32, name="at", tag="tp", bufs=TP_BUFS)
+                for jj in range(2):
+                    for u in range(2):
+                        nc.tensor.transpose(
+                            bank[:, jj, u, :], asorted[n][:, 2 * jp + jj, u, :], ident[:]
+                        )
                 banks.append(bank)
+            return banks
+
+        def gate_features(n, gt, banks):
             yg = sb.tile([P, BLK, 4], BF16, name="yg", tag="yg", bufs=2, align_bytes=64)
             for j in range(4):
+                jp, jj = divmod(j, 2)
                 nc.vector.tensor_tensor(
-                    out=yg[:, P * j : P * (j + 1), :],
-                    in0=gt[:, :, P * j : P * (j + 1)].rearrange("p t r -> p r t"),
-                    in1=banks[j][:].rearrange("p t r -> p r t"),
+                    out=yg[:, P * j : P * (j + 1), :].rearrange("p r (u e) -> p r u e", e=2),
+                    in0=banks[jp][:, jj, :, :].bitcast(BF16).rearrange("p u (r e) -> p r u e", e=2),
+                    in1=gt[:, :, P * j : P * (j + 1)].rearrange("p (u e) r -> p r u e", e=2),
                     op=MULT,
                 )
             return yg
@@ -262,7 +306,7 @@ def tile_attention_pb_l_kernel(tc, attn_out, hg_lin, x, Wg, bg, bhg, Wo, out):
             codes, scales = yq[blk]
             cols = slice(512 * oc, 512 * (oc + 1))
             for j in range(4):
-                acc = ps.tile([P, 512], F32, name="acc", tag="acc", bufs=4)
+                acc = ps.tile([P, 512], F32, name="acc", tag="acc", bufs=ACC_BUFS)
                 toks = slice(P * j, P * (j + 1))
                 for g in range(4):
                     nc.tensor.matmul_mx(
@@ -278,7 +322,7 @@ def tile_attention_pb_l_kernel(tc, attn_out, hg_lin, x, Wg, bg, bhg, Wo, out):
                 nc.scalar.copy(out=ot[:], in_=acc[:])
                 nc.sync.dma_start(out=out_v[b, i, j][:, cols], in_=ot[:])
 
-        hl = sb.tile([P, NBLK, 4 * H], BF16, name="hl", tag="xo", bufs=1)
+        hl = sb.tile([P, NBLK, 4 * H], BF16, name="hl", tag="xo", bufs=2)
         nc.scalar.dma_start(out=hl[:], in_=hg_v)
         nc.scalar.dma_start(out=bh[:], in_=bhg.partition_broadcast(P))
         nc.scalar.dma_start(out=bgb[:], in_=bg_v)
@@ -289,35 +333,25 @@ def tile_attention_pb_l_kernel(tc, attn_out, hg_lin, x, Wg, bg, bhg, Wo, out):
         nc.vector.memset(warm[:], 0.0)
         nc.scalar.activation(out=warm2[:], in_=warm[:], func=SIGMOID)
         nc.vector.tensor_copy(out=bgt[:], in_=bgb[:].rearrange("p g t -> p (g t)"))
-
-        def head_gates(lo, hi):
-            nc.vector.tensor_tensor(
-                out=hgs[:, lo:hi, :],
-                in0=hl[:].rearrange("p a (j h) -> p (a j) h", j=4)[:, lo:hi, :],
-                in1=bh[:].unsqueeze(1).to_broadcast([P, hi - lo, H]),
-                op=ADD,
-            )
-            nc.scalar.activation(out=hgs[:, lo:hi, :], in_=hgs[:, lo:hi, :], func=SIGMOID)
-
         head_gates(0, 12)
-        sort_x(0)
+        spread_gates(0)
+        transpose_gates(0)
         transpose_x(0)
-        quantize_x()
-        sort_x(1)
         transpose_x(1)
         w0 = group_w(nc.vector.tensor_copy, "wg", 0, 0)
         quantize_x()
+        transpose_x(2)
+        transpose_x(3)
         w1 = group_w(nc.vector.tensor_copy, "wg", 0, 1)
-        w2 = group_w(nc.scalar.copy, "wg", 0, 2)
-        w3 = group_w(nc.scalar.copy, "wg", 0, 3)
+        quantize_x()
         quantize_w("wg", 0, 0, w0)
+        w2 = group_w(nc.vector.tensor_copy, "wg", 0, 2)
+        w3 = group_w(nc.scalar.copy, "wg", 0, 3)
         quantize_w("wg", 0, 1, w1)
         quantize_w("wg", 0, 2, w2)
         quantize_w("wg", 0, 3, w3)
-        for j in range(4):
-            gate_heads(0, j)
+        sort_a(0)
         fetch_x()
-        sort_x(2)
 
         for s in range(NSTEP + LAG):
             fetch()
@@ -325,8 +359,7 @@ def tile_attention_pb_l_kernel(tc, attn_out, hg_lin, x, Wg, bg, bhg, Wo, out):
             quantize_x()
             if s == 5:
                 head_gates(12, 4 * NBLK)
-            if s % 2 == 1 and (s + 5) // 2 < 2 * NBLK:
-                sort_x((s + 5) // 2)
+            sort_x(s + 6)
             chunk = None
             if s < 3:
                 chunk = ("wg", s + 1)
@@ -339,21 +372,23 @@ def tile_attention_pb_l_kernel(tc, attn_out, hg_lin, x, Wg, bg, bhg, Wo, out):
                 nv = NV[s]
                 early = [group_w(nc.vector.tensor_copy, kind, c, g) for g in range(nv)]
                 extra = [(kind, c, g) for g in range(nv, 4)]
-            for j in range(4):
-                if s + 1 < NSTEP:
-                    gate_heads(s + 1, j)
-                if j < len(early):
-                    quantize_w(kind, c, j, early[j])
+            spread_gates(s + 1)
+            sort_a(s + 1)
+            for q in range(len(early)):
+                quantize_w(kind, c, q, early[q])
             fetch()
             if s < NSTEP:
                 gt, late = stage1(s, extra)
                 fetch()
                 for q in range(len(late)):
                     quantize_w(kind, c, len(early) + q, late[q])
-                yg = gate_features(s, gt)
+                transpose_gates(s + 1)
+                if s == 0:
+                    transpose_x(4)
+                transpose_x(s + 5)
+                banks = transpose_a(s)
+                yg = gate_features(s, gt, banks)
             if s >= LAG:
                 stage2(s - LAG)
             if s < NSTEP:
                 quantize_y(s, yg)
-            if s % 2 == 0 and s // 2 + 2 < 2 * NBLK:
-                transpose_x(s // 2 + 2)

@@ -25,8 +25,8 @@ LAG = 4
 RAW_BUFS = 6
 NV = [2, 2, 2, 2, 2, 2, 2]
 SORT_FROM = 12
-TP_BUFS = 5
-ACC_BUFS = 3
+TP_BUFS = 4
+ACC_BUFS = 4
 
 
 def tile_attention_pb_l_kernel(tc, attn_out, hg_lin, x, Wg, bg, bhg, Wo, out):
@@ -51,7 +51,6 @@ def tile_attention_pb_l_kernel(tc, attn_out, hg_lin, x, Wg, bg, bhg, Wo, out):
         wgs = keep.tile([P, 4, HD], U8, name="wgs", align_bytes=64)
         woq = keep.tile([P, 4, DIM], U32, name="woq", align_bytes=64)
         wos = keep.tile([P, 4, DIM], U8, name="wos", align_bytes=64)
-        hgs = keep.tile([P, 4 * NBLK, H], F32, name="hgs")
         bh = keep.tile([P, H], BF16, name="bh")
         bgb = keep.tile([P, 4, 4], BF16, name="bgb")
         bgt = keep.tile([P, 16], F32, name="bgt")
@@ -72,7 +71,6 @@ def tile_attention_pb_l_kernel(tc, attn_out, hg_lin, x, Wg, bg, bhg, Wo, out):
         xq = {}
         yq = {}
         asorted = {}
-        spread = {}
         gateT = {}
         state = {"next": 0, "used": 0, "xnext": 0, "xused": 0, "pending": []}
 
@@ -184,14 +182,18 @@ def tile_attention_pb_l_kernel(tc, attn_out, hg_lin, x, Wg, bg, bhg, Wo, out):
                 out=codes[:, g, cols].bitcast(FP8X4), scales=scales[:, g, cols], in_=wgp[:]
             )
 
-        def head_gates(lo, hi):
-            nc.vector.tensor_tensor(
-                out=hgs[:, lo:hi, :],
-                in0=hl[:].rearrange("p a (j h) -> p (a j) h", j=4)[:, lo:hi, :],
-                in1=bh[:].unsqueeze(1).to_broadcast([P, hi - lo, H]),
-                op=ADD,
-            )
-            nc.scalar.activation(out=hgs[:, lo:hi, :], in_=hgs[:, lo:hi, :], func=SIGMOID)
+        def fetch_gates(hb):
+            if hb >= 2 * NBLK:
+                return
+            blk, hf = divmod(hb, 2)
+            t = sb.tile([P, 2, BLK], F32, name="hgT", tag="hgT", bufs=3)
+            for hl8 in range(8):
+                rows = park[blk, 16 * hl8 + 8 * hf : 16 * hl8 + 8 * hf + 8, :]
+                nc.sync.dma_start(
+                    out=t[16 * hl8 : 16 * hl8 + 16, :, :].rearrange("p g n -> p (g n)"),
+                    in_=rows.rearrange("q r -> (q r)").partition_broadcast(16),
+                )
+            gateT[hb] = t
 
         def sort_a(n):
             if n >= NSTEP:
@@ -206,29 +208,6 @@ def tile_attention_pb_l_kernel(tc, attn_out, hg_lin, x, Wg, bg, bhg, Wo, out):
                 )
             asorted[n] = ao
             state["used"] = state["used"] + 1
-
-        def spread_gates(n):
-            if n >= NSTEP:
-                return
-            blk, grp = divmod(n, 4)
-            sp = sb.tile([P, 4, P], F32, name="sp", tag="sp", bufs=2)
-            nc.vector.tensor_copy(
-                out=sp[:].rearrange("p j (h r) -> p j h r", h=8),
-                in_=hgs[:, 4 * blk : 4 * blk + 4, 8 * grp : 8 * grp + 8]
-                .unsqueeze(3)
-                .to_broadcast([P, 4, 8, 16]),
-            )
-            spread[n] = sp
-
-        def transpose_gates(n):
-            if n >= NSTEP:
-                return
-            bank = ps.tile([P, 4, P], F32, name="ht", tag="tp", bufs=TP_BUFS)
-            for j in range(4):
-                nc.tensor.transpose(bank[:, j, :], spread[n][:, j, :], ident[:])
-            hgT = sb.tile([P, BLK], F32, name="hgT", tag="hgT", bufs=2)
-            nc.scalar.copy(out=hgT[:], in_=bank[:].rearrange("p j r -> p (j r)"))
-            gateT[n] = hgT
 
         def stage1(n, extra):
             blk, grp = divmod(n, 4)
@@ -256,7 +235,7 @@ def tile_attention_pb_l_kernel(tc, attn_out, hg_lin, x, Wg, bg, bhg, Wo, out):
                     scale=1.0,
                 )
                 nc.vector.tensor_tensor(
-                    out=gt[:, t, :], in0=gt[:, t, :], in1=gateT[n][:], op=MULT
+                    out=gt[:, t, :], in0=gt[:, t, :], in1=gateT[n // 2][:, n % 2, :], op=MULT
                 )
                 if t < len(extra):
                     kind, c, g = extra[t]
@@ -322,6 +301,9 @@ def tile_attention_pb_l_kernel(tc, attn_out, hg_lin, x, Wg, bg, bhg, Wo, out):
                 nc.scalar.copy(out=ot[:], in_=acc[:])
                 nc.sync.dma_start(out=out_v[b, i, j][:, cols], in_=ot[:])
 
+        park = out[B - 1, N - 96 : N, :].rearrange("a (c r) -> (a c) r", r=P).rearrange(
+            "(k q) r -> k q r", q=P
+        )
         hl = sb.tile([P, NBLK, 4 * H], BF16, name="hl", tag="xo", bufs=2)
         nc.scalar.dma_start(out=hl[:], in_=hg_v)
         nc.scalar.dma_start(out=bh[:], in_=bhg.partition_broadcast(P))
@@ -333,9 +315,31 @@ def tile_attention_pb_l_kernel(tc, attn_out, hg_lin, x, Wg, bg, bhg, Wo, out):
         nc.vector.memset(warm[:], 0.0)
         nc.scalar.activation(out=warm2[:], in_=warm[:], func=SIGMOID)
         nc.vector.tensor_copy(out=bgt[:], in_=bgb[:].rearrange("p g t -> p (g t)"))
-        head_gates(0, 12)
-        spread_gates(0)
-        transpose_gates(0)
+        hgs = sb.tile([P, NBLK, 4, H], F32, name="hgs", tag="g", bufs=2)
+        nc.vector.tensor_tensor(
+            out=hgs[:].rearrange("p a j h -> p (a j) h"),
+            in0=hl[:].rearrange("p a (j h) -> p (a j) h", j=4),
+            in1=bh[:].unsqueeze(1).to_broadcast([P, 4 * NBLK, H]),
+            op=ADD,
+        )
+        nc.scalar.activation(out=hgs[:], in_=hgs[:], func=SIGMOID)
+        hgp = sb.tile([P, NBLK, P], F32, name="hgp", tag="g", bufs=2)
+        for blk in range(NBLK):
+            nc.vector.tensor_copy(
+                out=hgp[:, blk, :].rearrange("p (h g j) -> p h g j", h=8, g=4),
+                in_=hgs[:, blk, :, :].rearrange("p j (g h) -> p h g j", g=4),
+            )
+        hT = sb.tile([P, NBLK, P], F32, name="hT", tag="yq", bufs=2, align_bytes=64)
+        for b3 in range(3):
+            bank = ps.tile([P, 4, P], F32, name="ht", tag="tp", bufs=TP_BUFS)
+            for q in range(4):
+                nc.tensor.transpose(bank[:, q, :], hgp[:, 4 * b3 + q, :], ident[:])
+            nc.scalar.copy(out=hT[:, 4 * b3 : 4 * b3 + 4, :], in_=bank[:])
+            nc.scalar.dma_start(
+                out=park[4 * b3 : 4 * b3 + 4].rearrange("k q r -> q k r"),
+                in_=hT[:, 4 * b3 : 4 * b3 + 4, :],
+            )
+        fetch_gates(0)
         transpose_x(0)
         transpose_x(1)
         w0 = group_w(nc.vector.tensor_copy, "wg", 0, 0)
@@ -357,8 +361,8 @@ def tile_attention_pb_l_kernel(tc, attn_out, hg_lin, x, Wg, bg, bhg, Wo, out):
             fetch()
             fetch_x()
             quantize_x()
-            if s == 5:
-                head_gates(12, 4 * NBLK)
+            if s % 2 == 0:
+                fetch_gates(s // 2 + 1)
             sort_x(s + 6)
             chunk = None
             if s < 3:
@@ -372,7 +376,6 @@ def tile_attention_pb_l_kernel(tc, attn_out, hg_lin, x, Wg, bg, bhg, Wo, out):
                 nv = NV[s]
                 early = [group_w(nc.vector.tensor_copy, kind, c, g) for g in range(nv)]
                 extra = [(kind, c, g) for g in range(nv, 4)]
-            spread_gates(s + 1)
             sort_a(s + 1)
             for q in range(len(early)):
                 quantize_w(kind, c, q, early[q])
@@ -382,7 +385,6 @@ def tile_attention_pb_l_kernel(tc, attn_out, hg_lin, x, Wg, bg, bhg, Wo, out):
                 fetch()
                 for q in range(len(late)):
                     quantize_w(kind, c, len(early) + q, late[q])
-                transpose_gates(s + 1)
                 if s == 0:
                     transpose_x(4)
                 transpose_x(s + 5)

@@ -17,16 +17,19 @@ ADD = mybir.AluOpType.add
 SIGMOID = mybir.ActivationFunctionType.Sigmoid
 
 P = 128
-BLK = 512
-NBLK = B * N // BLK
-BLK_PER_B = N // BLK
-NSTEP = 4 * NBLK
-LAG = 4
+PACK = 4
+WIDE = 512
+PASSES = DIM // WIDE
+BLOCKS = B * N // WIDE
+BLOCKS_PER_BATCH = N // WIDE
+STEPS = PASSES * BLOCKS
+LAG = PASSES
+X_AHEAD = 5
+SORTED_FROM = 12
 RAW_BUFS = 6
-NV = [2, 2, 2, 2, 2, 2, 2]
-SORT_FROM = 12
-TP_BUFS = 4
-ACC_BUFS = 4
+VECTOR_SHARE = 2
+WEIGHT_STEPS = 2 * PASSES - 1
+PARK_ROWS = BLOCKS * P * P // DIM
 
 
 def tile_attention_pb_l_kernel(tc, attn_out, hg_lin, x, Wg, bg, bhg, Wo, out):
@@ -36,9 +39,12 @@ def tile_attention_pb_l_kernel(tc, attn_out, hg_lin, x, Wg, bg, bhg, Wo, out):
     a_v = attn_out.rearrange("b h (i p j) d -> b i p h (j d)", p=P, j=4)
     hg_v = hg_lin.rearrange("b (i p j) h -> p (b i) (j h)", p=P, j=4)
     out_v = out.rearrange("b (i r j) c -> b i j r c", r=P, j=4)
-    wg_v = Wg.rearrange("(g p j) c -> g p j c", p=P, j=4)
-    wo_v = Wo.rearrange("(g p j) c -> g p j c", p=P, j=4)
-    bg_v = bg.rearrange("(g p t) -> p g t", p=P, t=4)
+    wg_v = Wg.rearrange("(g p j) c -> g p j c", p=P, j=PACK)
+    wo_v = Wo.rearrange("(g p j) c -> g p j c", p=P, j=PACK)
+    bg_v = bg.rearrange("(g p t) -> p g t", p=P, t=PACK)
+    park = out[B - 1, N - PARK_ROWS : N, :].rearrange("a (c r) -> (a c) r", r=P).rearrange(
+        "(k q) r -> k q r", q=P
+    )
 
     with ExitStack() as ctx:
         keep = ctx.enter_context(tc.tile_pool(name="keep", bufs=1))
@@ -47,94 +53,94 @@ def tile_attention_pb_l_kernel(tc, attn_out, hg_lin, x, Wg, bg, bhg, Wo, out):
         ctx.enter_context(tc.manual_schedule())
 
         ident = keep.tile([P, P], F32, name="ident")
-        wgq = keep.tile([P, 4, HD], U32, name="wgq", align_bytes=64)
-        wgs = keep.tile([P, 4, HD], U8, name="wgs", align_bytes=64)
-        woq = keep.tile([P, 4, DIM], U32, name="woq", align_bytes=64)
-        wos = keep.tile([P, 4, DIM], U8, name="wos", align_bytes=64)
+        wgq = keep.tile([P, PASSES, HD], U32, name="wgq", align_bytes=64)
+        wgs = keep.tile([P, PASSES, HD], U8, name="wgs", align_bytes=64)
+        woq = keep.tile([P, PASSES, DIM], U32, name="woq", align_bytes=64)
+        wos = keep.tile([P, PASSES, DIM], U8, name="wos", align_bytes=64)
         bh = keep.tile([P, H], BF16, name="bh")
-        bgb = keep.tile([P, 4, 4], BF16, name="bgb")
-        bgt = keep.tile([P, 16], F32, name="bgt")
+        bgb = keep.tile([P, PASSES, PACK], BF16, name="bgb")
+        bgt = keep.tile([P, PASSES * PACK], F32, name="bgt")
         warm = keep.tile([P, 1], F32, name="warm")
         warm2 = keep.tile([P, 1], F32, name="warm2")
 
-        order = [("wg", 0, g) for g in range(4)] + [("a", 0, 0)]
-        for q in range(7):
-            kind, c = ("wg", q + 1) if q < 3 else ("wo", q - 3)
-            order.extend([(kind, c, g) for g in range(NV[q])])
-            order.append(("a", q + 1, 0))
-            order.extend([(kind, c, g) for g in range(NV[q], 4)])
-        order.extend([("a", n, 0) for n in range(8, NSTEP)])
+        loads = [("wg", 0, kp) for kp in range(PASSES)] + [("a", 0, 0)]
+        for s in range(WEIGHT_STEPS):
+            kind, chunk = ("wg", s + 1) if s + 1 < PASSES else ("wo", s + 1 - PASSES)
+            loads.extend([(kind, chunk, kp) for kp in range(VECTOR_SHARE)])
+            loads.append(("a", s + 1, 0))
+            loads.extend([(kind, chunk, kp) for kp in range(VECTOR_SHARE, PASSES)])
+        loads.extend([("a", sg, 0) for sg in range(WEIGHT_STEPS + 1, STEPS)])
 
         raw = {}
-        xraw = {}
-        xsorted = {}
-        xq = {}
-        yq = {}
-        asorted = {}
-        gateT = {}
-        state = {"next": 0, "used": 0, "xnext": 0, "xused": 0, "pending": []}
+        x_raw = {}
+        x_sorted = {}
+        x_codes = {}
+        y_codes = {}
+        a_sorted = {}
+        head_gates = {}
+        state = {"issued": 0, "read": 0, "x_issued": 0, "x_read": 0, "to_quantize": []}
 
         def fetch():
-            lo = state["next"]
-            hi = min(len(order), state["used"] + RAW_BUFS)
-            for q in range(lo, hi):
-                kind, c, g = order[q]
-                t = sb.tile([P, 2048], BF16, name="raw", tag="raw", bufs=RAW_BUFS)
+            first = state["issued"]
+            last = min(len(loads), state["read"] + RAW_BUFS)
+            for q in range(first, last):
+                kind, number, kp = loads[q]
+                tile = sb.tile([P, 2048], BF16, name="raw", tag="raw", bufs=RAW_BUFS)
                 if kind == "a":
-                    blk, grp = divmod(c, 4)
-                    b, i = divmod(blk, BLK_PER_B)
+                    blk, grp = divmod(number, PASSES)
+                    b, i = divmod(blk, BLOCKS_PER_BATCH)
                     nc.sync.dma_start(
-                        out=t[:].rearrange("p (h e) -> p h e", h=8),
+                        out=tile[:].rearrange("p (h e) -> p h e", h=8),
                         in_=a_v[b, i][:, 8 * grp : 8 * grp + 8, :],
                     )
                 else:
                     src = wg_v if kind == "wg" else wo_v
                     nc.sync.dma_start(
-                        out=t[:].rearrange("p (j c) -> p j c", j=4),
-                        in_=src[g][:, :, 512 * c : 512 * (c + 1)],
+                        out=tile[:].rearrange("p (j c) -> p j c", j=PACK),
+                        in_=src[kp][:, :, WIDE * number : WIDE * (number + 1)],
                     )
-                raw[(kind, c, g)] = t
-            state["next"] = max(lo, hi)
+                raw[(kind, number, kp)] = tile
+            state["issued"] = max(first, last)
 
         def fetch_x():
-            m = state["xnext"]
-            if m < 2 * NBLK and m < state["xused"] + 2:
-                blk, h = divmod(m, 2)
-                b, i = divmod(blk, BLK_PER_B)
-                t = sb.tile([P, 4, 1024], BF16, name="xr", tag="xr", bufs=2)
-                nc.sync.dma_start(out=t[:], in_=x_v[b, i][:, :, 1024 * h : 1024 * (h + 1)])
-                xraw[m] = t
-                state["xnext"] = m + 1
+            half = state["x_issued"]
+            if half < 2 * BLOCKS and half < state["x_read"] + 2:
+                blk, side = divmod(half, 2)
+                b, i = divmod(blk, BLOCKS_PER_BATCH)
+                tile = sb.tile([P, 4, 1024], BF16, name="xr", tag="xr", bufs=2)
+                nc.sync.dma_start(out=tile[:], in_=x_v[b, i][:, :, 1024 * side : 1024 * (side + 1)])
+                x_raw[half] = tile
+                state["x_issued"] = half + 1
 
-        def sort_x(q):
-            if q < SORT_FROM or q >= NSTEP:
+        def sort_x(xp):
+            if xp < SORTED_FROM or xp >= STEPS:
                 return
-            m, gl = divmod(q, 2)
-            words = xraw[m][:].rearrange("p j k -> p (j k)").bitcast(F32)
+            half, side = divmod(xp, 2)
+            words = x_raw[half][:].rearrange("p j k -> p (j k)").bitcast(F32)
             xo = sb.tile([P, 4, 2, P], F32, name="xo", tag="xo", bufs=2)
             nc.vector.tensor_copy(
                 out=xo[:],
-                in_=words.rearrange("p (j g w u) -> p j g u w", j=4, g=2, u=2)[:, :, gl, :, :],
+                in_=words.rearrange("p (j g w u) -> p j g u w", j=4, g=2, u=2)[:, :, side, :, :],
             )
-            xsorted[q] = xo
-            if gl == 1:
-                state["xused"] = m + 1
+            x_sorted[xp] = xo
+            if side == 1:
+                state["x_read"] = half + 1
 
-        def transpose_x(q):
-            if q >= NSTEP:
+        def transpose_x(xp):
+            if xp >= STEPS:
                 return
-            m, gl = divmod(q, 2)
+            half, side = divmod(xp, 2)
             xg = sb.tile([P, 2048], BF16, name="xg", tag="grp", bufs=4, align_bytes=64)
             xgw = xg[:].bitcast(F32).rearrange("p (n u) -> p n u", u=2)
             for jp in range(2):
-                bank = ps.tile([P, 2, 2, P], F32, name="xt", tag="tp", bufs=TP_BUFS)
+                bank = ps.tile([P, 2, 2, P], F32, name="xt", tag="tp", bufs=4)
                 for jj in range(2):
                     for u in range(2):
-                        if q < SORT_FROM:
-                            words = xraw[m][:, 2 * jp + jj, :].bitcast(F32)
-                            piece = words[:, 256 * gl + u : 256 * (gl + 1) : 2]
+                        if xp < SORTED_FROM:
+                            words = x_raw[half][:, 2 * jp + jj, :].bitcast(F32)
+                            piece = words[:, 256 * side + u : 256 * (side + 1) : 2]
                         else:
-                            piece = xsorted[q][:, 2 * jp + jj, u, :]
+                            piece = x_sorted[xp][:, 2 * jp + jj, u, :]
                         nc.tensor.transpose(bank[:, jj, u, :], piece, ident[:])
                 nc.scalar.copy(
                     out=xgw[:, 256 * jp : 256 * (jp + 1), :].rearrange(
@@ -142,63 +148,63 @@ def tile_attention_pb_l_kernel(tc, attn_out, hg_lin, x, Wg, bg, bhg, Wo, out):
                     ),
                     in_=bank[:].rearrange("p jj u r -> p jj r u"),
                 )
-            state["pending"].append((q, xg))
-            if q < SORT_FROM and gl == 1:
-                state["xused"] = m + 1
+            state["to_quantize"].append((xp, xg))
+            if xp < SORTED_FROM and side == 1:
+                state["x_read"] = half + 1
 
         def quantize_x():
-            for q, xg in state["pending"]:
-                blk, g = divmod(q, 4)
-                if g == 0:
-                    codes = sb.tile([P, 4, BLK], U32, name="xq", tag="xq", bufs=2, align_bytes=64)
-                    scales = sb.tile([P, 4, BLK], U8, name="xs", tag="xs", bufs=2, align_bytes=64)
-                    xq[blk] = (codes, scales)
-                codes, scales = xq[blk]
+            for xp, xg in state["to_quantize"]:
+                blk, kp = divmod(xp, PASSES)
+                if kp == 0:
+                    codes = sb.tile([P, PASSES, WIDE], U32, name="xq", tag="xq", bufs=2, align_bytes=64)
+                    scales = sb.tile([P, PASSES, WIDE], U8, name="xs", tag="xs", bufs=2, align_bytes=64)
+                    x_codes[blk] = (codes, scales)
+                codes, scales = x_codes[blk]
                 nc.vector.quantize_mx(
-                    out=codes[:, g, :].bitcast(FP8X4), scales=scales[:, g, :], in_=xg[:]
+                    out=codes[:, kp, :].bitcast(FP8X4), scales=scales[:, kp, :], in_=xg[:]
                 )
-            state["pending"] = []
+            state["to_quantize"] = []
 
-        def group_w(copy, kind, c, g):
-            wr = raw[(kind, c, g)]
-            wgp = sb.tile([P, 2048], BF16, name="wgp", tag="grp", bufs=4, align_bytes=64)
+        def group_weights(copy, kind, chunk, kp):
+            rows = raw[(kind, chunk, kp)]
+            grouped = sb.tile([P, 2048], BF16, name="wgp", tag="grp", bufs=4, align_bytes=64)
             if kind == "wg":
                 copy(
-                    out=wgp[:].rearrange("p (t m j) -> p t m j", t=4, j=4),
-                    in_=wr[:].rearrange("p (j m t) -> p t m j", j=4, t=4),
+                    out=grouped[:].rearrange("p (t m j) -> p m j t", t=PACK, j=PACK),
+                    in_=rows[:].rearrange("p (j m t) -> p m j t", j=PACK, t=PACK),
                 )
             else:
                 copy(
-                    out=wgp[:].rearrange("p (n j) -> p n j", j=4),
-                    in_=wr[:].rearrange("p (j n) -> p n j", j=4),
+                    out=grouped[:].rearrange("p (c i j) -> p c j i", i=4, j=PACK),
+                    in_=rows[:].rearrange("p (j c i) -> p c j i", j=PACK, i=4),
                 )
-            state["used"] = state["used"] + 1
-            return wgp
+            state["read"] = state["read"] + 1
+            return grouped
 
-        def quantize_w(kind, c, g, wgp):
+        def quantize_weights(kind, chunk, kp, grouped):
             codes, scales = (wgq, wgs) if kind == "wg" else (woq, wos)
-            cols = slice(512 * c, 512 * (c + 1))
+            cols = slice(WIDE * chunk, WIDE * (chunk + 1))
             nc.vector.quantize_mx(
-                out=codes[:, g, cols].bitcast(FP8X4), scales=scales[:, g, cols], in_=wgp[:]
+                out=codes[:, kp, cols].bitcast(FP8X4), scales=scales[:, kp, cols], in_=grouped[:]
             )
 
-        def fetch_gates(hb):
-            if hb >= 2 * NBLK:
+        def fetch_head_gates(pair):
+            if pair >= 2 * BLOCKS:
                 return
-            blk, hf = divmod(hb, 2)
-            t = sb.tile([P, 2, BLK], F32, name="hgT", tag="hgT", bufs=3)
-            for hl8 in range(8):
-                rows = park[blk, 16 * hl8 + 8 * hf : 16 * hl8 + 8 * hf + 8, :]
+            blk, side = divmod(pair, 2)
+            tile = sb.tile([P, 2, WIDE], F32, name="hgT", tag="hgT", bufs=3)
+            for hl in range(8):
+                rows = park[blk, 16 * hl + 8 * side : 16 * hl + 8 * side + 8, :]
                 nc.sync.dma_start(
-                    out=t[16 * hl8 : 16 * hl8 + 16, :, :].rearrange("p g n -> p (g n)"),
+                    out=tile[16 * hl : 16 * hl + 16, :, :].rearrange("p g n -> p (g n)"),
                     in_=rows.rearrange("q r -> (q r)").partition_broadcast(16),
                 )
-            gateT[hb] = t
+            head_gates[pair] = tile
 
-        def sort_a(n):
-            if n >= NSTEP:
+        def sort_a(sg):
+            if sg >= STEPS:
                 return
-            words = raw[("a", n, 0)][:].bitcast(F32).rearrange(
+            words = raw[("a", sg, 0)][:].bitcast(F32).rearrange(
                 "p (h j m u) -> p u j h m", h=8, j=4, u=2
             )
             ao = sb.tile([P, 4, 2, P], F32, name="ao", tag="ao", bufs=2)
@@ -206,105 +212,102 @@ def tile_attention_pb_l_kernel(tc, attn_out, hg_lin, x, Wg, bg, bhg, Wo, out):
                 nc.vector.tensor_copy(
                     out=ao[:, :, u, :].rearrange("p j (h m) -> p j h m", h=8), in_=words[:, u]
                 )
-            asorted[n] = ao
-            state["used"] = state["used"] + 1
+            a_sorted[sg] = ao
+            state["read"] = state["read"] + 1
 
-        def stage1(n, extra):
-            blk, grp = divmod(n, 4)
-            codes, scales = xq[blk]
-            gt = sb.tile([P, 4, BLK], F32, name="gt", tag="g", bufs=2)
-            grouped = []
-            for t in range(4):
-                acc = ps.tile([P, BLK], F32, name="acc", tag="acc", bufs=ACC_BUFS)
-                cols = slice(512 * grp + P * t, 512 * grp + P * (t + 1))
-                for g in range(4):
+        def stage1(sg, scalar_share):
+            blk, grp = divmod(sg, PASSES)
+            codes, scales = x_codes[blk]
+            gates = sb.tile([P, PACK, WIDE], F32, name="gt", tag="g", bufs=2)
+            for t in range(PACK):
+                acc = ps.tile([P, WIDE], F32, name="acc", tag="acc", bufs=4)
+                cols = slice(WIDE * grp + P * t, WIDE * grp + P * (t + 1))
+                for kp in range(PASSES):
                     nc.tensor.matmul_mx(
                         out=acc[:],
-                        lhsT=wgq[:, g, cols].bitcast(FP8X4),
-                        lhsT_scale=wgs[:, g, cols],
-                        rhs=codes[:, g, :].bitcast(FP8X4),
-                        rhs_scale=scales[:, g, :],
-                        start=(g == 0),
-                        stop=(g == 3),
+                        lhsT=wgq[:, kp, cols].bitcast(FP8X4),
+                        lhsT_scale=wgs[:, kp, cols],
+                        rhs=codes[:, kp, :].bitcast(FP8X4),
+                        rhs_scale=scales[:, kp, :],
+                        start=(kp == 0),
+                        stop=(kp == PASSES - 1),
                     )
                 nc.scalar.activation(
-                    out=gt[:, t, :],
+                    out=gates[:, t, :],
                     in_=acc[:],
                     func=SIGMOID,
-                    bias=bgt[:, 4 * grp + t : 4 * grp + t + 1],
+                    bias=bgt[:, PACK * grp + t : PACK * grp + t + 1],
                     scale=1.0,
                 )
                 nc.vector.tensor_tensor(
-                    out=gt[:, t, :], in0=gt[:, t, :], in1=gateT[n // 2][:, n % 2, :], op=MULT
+                    out=gates[:, t, :],
+                    in0=gates[:, t, :],
+                    in1=head_gates[sg // 2][:, sg % 2, :],
+                    op=MULT,
                 )
-                if t < len(extra):
-                    kind, c, g = extra[t]
-                    grouped.append(group_w(nc.scalar.copy, kind, c, g))
-            return gt, grouped
+            done = [group_weights(nc.scalar.copy, *piece) for piece in scalar_share]
+            return gates, done
 
-        def transpose_a(n):
+        def transpose_a(sg):
             banks = []
             for jp in range(2):
-                bank = ps.tile([P, 2, 2, P], F32, name="at", tag="tp", bufs=TP_BUFS)
+                bank = ps.tile([P, 2, 2, P], F32, name="at", tag="tp", bufs=4)
                 for jj in range(2):
                     for u in range(2):
                         nc.tensor.transpose(
-                            bank[:, jj, u, :], asorted[n][:, 2 * jp + jj, u, :], ident[:]
+                            bank[:, jj, u, :], a_sorted[sg][:, 2 * jp + jj, u, :], ident[:]
                         )
                 banks.append(bank)
             return banks
 
-        def gate_features(n, gt, banks):
-            yg = sb.tile([P, BLK, 4], BF16, name="yg", tag="yg", bufs=2, align_bytes=64)
+        def multiply_y(gates, banks):
+            yg = sb.tile([P, WIDE, PACK], BF16, name="yg", tag="yg", bufs=2, align_bytes=64)
             for j in range(4):
                 jp, jj = divmod(j, 2)
                 nc.vector.tensor_tensor(
                     out=yg[:, P * j : P * (j + 1), :].rearrange("p r (u e) -> p r u e", e=2),
                     in0=banks[jp][:, jj, :, :].bitcast(BF16).rearrange("p u (r e) -> p r u e", e=2),
-                    in1=gt[:, :, P * j : P * (j + 1)].rearrange("p (u e) r -> p r u e", e=2),
+                    in1=gates[:, :, P * j : P * (j + 1)].rearrange("p (u e) r -> p r u e", e=2),
                     op=MULT,
                 )
             return yg
 
-        def quantize_y(n, yg):
-            blk, grp = divmod(n, 4)
+        def quantize_y(sg, yg):
+            blk, grp = divmod(sg, PASSES)
             if grp == 0:
-                codes = sb.tile([P, 4, BLK], U32, name="yq", tag="yq", bufs=2, align_bytes=64)
-                scales = sb.tile([P, 4, BLK], U8, name="ys", tag="ys", bufs=2, align_bytes=64)
-                yq[blk] = (codes, scales)
-            codes, scales = yq[blk]
+                codes = sb.tile([P, PASSES, WIDE], U32, name="yq", tag="yq", bufs=2, align_bytes=64)
+                scales = sb.tile([P, PASSES, WIDE], U8, name="ys", tag="ys", bufs=2, align_bytes=64)
+                y_codes[blk] = (codes, scales)
+            codes, scales = y_codes[blk]
             nc.vector.quantize_mx(
                 out=codes[:, grp, :].bitcast(FP8X4),
                 scales=scales[:, grp, :],
                 in_=yg[:].rearrange("p n t -> p (n t)"),
             )
 
-        def stage2(m):
-            blk, oc = divmod(m, 4)
-            b, i = divmod(blk, BLK_PER_B)
-            codes, scales = yq[blk]
-            cols = slice(512 * oc, 512 * (oc + 1))
+        def stage2(og):
+            blk, colgrp = divmod(og, PASSES)
+            b, i = divmod(blk, BLOCKS_PER_BATCH)
+            codes, scales = y_codes[blk]
+            cols = slice(WIDE * colgrp, WIDE * (colgrp + 1))
             for j in range(4):
-                acc = ps.tile([P, 512], F32, name="acc", tag="acc", bufs=ACC_BUFS)
+                acc = ps.tile([P, WIDE], F32, name="acc", tag="acc", bufs=4)
                 toks = slice(P * j, P * (j + 1))
-                for g in range(4):
+                for kp in range(PASSES):
                     nc.tensor.matmul_mx(
                         out=acc[:],
-                        lhsT=codes[:, g, toks].bitcast(FP8X4),
-                        lhsT_scale=scales[:, g, toks],
-                        rhs=woq[:, g, cols].bitcast(FP8X4),
-                        rhs_scale=wos[:, g, cols],
-                        start=(g == 0),
-                        stop=(g == 3),
+                        lhsT=codes[:, kp, toks].bitcast(FP8X4),
+                        lhsT_scale=scales[:, kp, toks],
+                        rhs=woq[:, kp, cols].bitcast(FP8X4),
+                        rhs_scale=wos[:, kp, cols],
+                        start=(kp == 0),
+                        stop=(kp == PASSES - 1),
                     )
-                ot = sb.tile([P, 512], F32, name="ot", tag="o", bufs=4)
+                ot = sb.tile([P, WIDE], F32, name="ot", tag="o", bufs=4)
                 nc.scalar.copy(out=ot[:], in_=acc[:])
                 nc.sync.dma_start(out=out_v[b, i, j][:, cols], in_=ot[:])
 
-        park = out[B - 1, N - 96 : N, :].rearrange("a (c r) -> (a c) r", r=P).rearrange(
-            "(k q) r -> k q r", q=P
-        )
-        hl = sb.tile([P, NBLK, 4 * H], BF16, name="hl", tag="xo", bufs=2)
+        hl = sb.tile([P, BLOCKS, 4 * H], BF16, name="hl", tag="xo", bufs=2)
         nc.scalar.dma_start(out=hl[:], in_=hg_v)
         nc.scalar.dma_start(out=bh[:], in_=bhg.partition_broadcast(P))
         nc.scalar.dma_start(out=bgb[:], in_=bg_v)
@@ -315,82 +318,82 @@ def tile_attention_pb_l_kernel(tc, attn_out, hg_lin, x, Wg, bg, bhg, Wo, out):
         nc.vector.memset(warm[:], 0.0)
         nc.scalar.activation(out=warm2[:], in_=warm[:], func=SIGMOID)
         nc.vector.tensor_copy(out=bgt[:], in_=bgb[:].rearrange("p g t -> p (g t)"))
-        hgs = sb.tile([P, NBLK, 4, H], F32, name="hgs", tag="g", bufs=2)
+
+        hgs = sb.tile([P, BLOCKS, 4, H], F32, name="hgs", tag="g", bufs=2)
         nc.vector.tensor_tensor(
             out=hgs[:].rearrange("p a j h -> p (a j) h"),
             in0=hl[:].rearrange("p a (j h) -> p (a j) h", j=4),
-            in1=bh[:].unsqueeze(1).to_broadcast([P, 4 * NBLK, H]),
+            in1=bh[:].unsqueeze(1).to_broadcast([P, 4 * BLOCKS, H]),
             op=ADD,
         )
         nc.scalar.activation(out=hgs[:], in_=hgs[:], func=SIGMOID)
-        hgp = sb.tile([P, NBLK, P], F32, name="hgp", tag="g", bufs=2)
-        for blk in range(NBLK):
+        hgp = sb.tile([P, BLOCKS, P], F32, name="hgp", tag="g", bufs=2)
+        for blk in range(BLOCKS):
             nc.vector.tensor_copy(
-                out=hgp[:, blk, :].rearrange("p (h g j) -> p h g j", h=8, g=4),
-                in_=hgs[:, blk, :, :].rearrange("p j (g h) -> p h g j", g=4),
+                out=hgp[:, blk, :].rearrange("p (h g j) -> p h g j", h=8, g=PASSES),
+                in_=hgs[:, blk, :, :].rearrange("p j (g h) -> p h g j", g=PASSES),
             )
-        hT = sb.tile([P, NBLK, P], F32, name="hT", tag="yq", bufs=2, align_bytes=64)
-        for b3 in range(3):
-            bank = ps.tile([P, 4, P], F32, name="ht", tag="tp", bufs=TP_BUFS)
+        hT = sb.tile([P, BLOCKS, P], F32, name="hT", tag="yq", bufs=2, align_bytes=64)
+        for first in range(0, BLOCKS, 4):
+            bank = ps.tile([P, 4, P], F32, name="ht", tag="tp", bufs=4)
             for q in range(4):
-                nc.tensor.transpose(bank[:, q, :], hgp[:, 4 * b3 + q, :], ident[:])
-            nc.scalar.copy(out=hT[:, 4 * b3 : 4 * b3 + 4, :], in_=bank[:])
+                nc.tensor.transpose(bank[:, q, :], hgp[:, first + q, :], ident[:])
+            nc.scalar.copy(out=hT[:, first : first + 4, :], in_=bank[:])
             nc.scalar.dma_start(
-                out=park[4 * b3 : 4 * b3 + 4].rearrange("k q r -> q k r"),
-                in_=hT[:, 4 * b3 : 4 * b3 + 4, :],
+                out=park[first : first + 4].rearrange("k q r -> q k r"),
+                in_=hT[:, first : first + 4, :],
             )
-        fetch_gates(0)
+
         transpose_x(0)
         transpose_x(1)
-        w0 = group_w(nc.vector.tensor_copy, "wg", 0, 0)
+        w0 = group_weights(nc.vector.tensor_copy, "wg", 0, 0)
         quantize_x()
         transpose_x(2)
         transpose_x(3)
-        w1 = group_w(nc.vector.tensor_copy, "wg", 0, 1)
+        w1 = group_weights(nc.vector.tensor_copy, "wg", 0, 1)
         quantize_x()
-        quantize_w("wg", 0, 0, w0)
-        w2 = group_w(nc.vector.tensor_copy, "wg", 0, 2)
-        w3 = group_w(nc.scalar.copy, "wg", 0, 3)
-        quantize_w("wg", 0, 1, w1)
-        quantize_w("wg", 0, 2, w2)
-        quantize_w("wg", 0, 3, w3)
+        quantize_weights("wg", 0, 0, w0)
+        w2 = group_weights(nc.vector.tensor_copy, "wg", 0, 2)
+        w3 = group_weights(nc.scalar.copy, "wg", 0, 3)
+        quantize_weights("wg", 0, 1, w1)
+        quantize_weights("wg", 0, 2, w2)
+        quantize_weights("wg", 0, 3, w3)
+        fetch()
+        fetch_head_gates(0)
         sort_a(0)
         fetch_x()
 
-        for s in range(NSTEP + LAG):
+        for s in range(STEPS + LAG):
             fetch()
             fetch_x()
             quantize_x()
             if s % 2 == 0:
-                fetch_gates(s // 2 + 1)
-            sort_x(s + 6)
-            chunk = None
-            if s < 3:
-                chunk = ("wg", s + 1)
-            elif s < 7:
-                chunk = ("wo", s - 3)
-            extra = []
-            early = []
-            if chunk is not None:
-                kind, c = chunk
-                nv = NV[s]
-                early = [group_w(nc.vector.tensor_copy, kind, c, g) for g in range(nv)]
-                extra = [(kind, c, g) for g in range(nv, 4)]
+                fetch_head_gates(s // 2 + 1)
+            sort_x(s + X_AHEAD + 1)
+            vector_share = []
+            scalar_share = []
+            if s < WEIGHT_STEPS:
+                kind, chunk = ("wg", s + 1) if s + 1 < PASSES else ("wo", s + 1 - PASSES)
+                vector_share = [
+                    group_weights(nc.vector.tensor_copy, kind, chunk, kp)
+                    for kp in range(VECTOR_SHARE)
+                ]
+                scalar_share = [(kind, chunk, kp) for kp in range(VECTOR_SHARE, PASSES)]
             sort_a(s + 1)
-            for q in range(len(early)):
-                quantize_w(kind, c, q, early[q])
+            for kp in range(len(vector_share)):
+                quantize_weights(kind, chunk, kp, vector_share[kp])
             fetch()
-            if s < NSTEP:
-                gt, late = stage1(s, extra)
+            if s < STEPS:
+                gates, done = stage1(s, scalar_share)
                 fetch()
-                for q in range(len(late)):
-                    quantize_w(kind, c, len(early) + q, late[q])
+                for q in range(len(done)):
+                    quantize_weights(kind, chunk, VECTOR_SHARE + q, done[q])
                 if s == 0:
-                    transpose_x(4)
-                transpose_x(s + 5)
+                    transpose_x(X_AHEAD - 1)
+                transpose_x(s + X_AHEAD)
                 banks = transpose_a(s)
-                yg = gate_features(s, gt, banks)
+                yg = multiply_y(gates, banks)
             if s >= LAG:
                 stage2(s - LAG)
-            if s < NSTEP:
+            if s < STEPS:
                 quantize_y(s, yg)

from contextlib import ExitStack

import concourse.mybir as mybir
from concourse.masks import make_identity

B, N, DIM, H, D = 2, 3072, 2048, 32, 64
HD = H * D
FLOPS = 2 * B * N * DIM * HD + 2 * B * N * HD * DIM

F32 = mybir.dt.float32
BF16 = mybir.dt.bfloat16
U32 = mybir.dt.uint32
U8 = mybir.dt.uint8
FP8X4 = mybir.dt.float8_e4m3fn_x4
MULT = mybir.AluOpType.mult
ADD = mybir.AluOpType.add
SIGMOID = mybir.ActivationFunctionType.Sigmoid

P = 128
PACK = 4
WIDE = 512
PASSES = DIM // WIDE
BLOCKS = B * N // WIDE
BLOCKS_PER_BATCH = N // WIDE
STEPS = PASSES * BLOCKS
LAG = PASSES
X_AHEAD = 5
SORTED_FROM = 12
RAW_BUFS = 6
VECTOR_SHARE = 2
WEIGHT_STEPS = 2 * PASSES - 1
PARK_ROWS = BLOCKS * P * P // DIM


def tile_attention_pb_l_kernel(tc, attn_out, hg_lin, x, Wg, bg, bhg, Wo, out):
    nc = tc.nc

    x_v = x.rearrange("b (i p j) k -> b i p j k", p=P, j=4)
    a_v = attn_out.rearrange("b h (i p j) d -> b i p h (j d)", p=P, j=4)
    hg_v = hg_lin.rearrange("b (i p j) h -> p (b i) (j h)", p=P, j=4)
    out_v = out.rearrange("b (i r j) c -> b i j r c", r=P, j=4)
    wg_v = Wg.rearrange("(g p j) c -> g p j c", p=P, j=PACK)
    wo_v = Wo.rearrange("(g p j) c -> g p j c", p=P, j=PACK)
    bg_v = bg.rearrange("(g p t) -> p g t", p=P, t=PACK)
    park = out[B - 1, N - PARK_ROWS : N, :].rearrange("a (c r) -> (a c) r", r=P).rearrange(
        "(k q) r -> k q r", q=P
    )

    with ExitStack() as ctx:
        keep = ctx.enter_context(tc.tile_pool(name="keep", bufs=1))
        sb = ctx.enter_context(tc.tile_pool(name="sb", bufs=2))
        ps = ctx.enter_context(tc.psum_pool(name="ps", bufs=4))
        ctx.enter_context(tc.manual_schedule())

        ident = keep.tile([P, P], F32, name="ident")
        wgq = keep.tile([P, PASSES, HD], U32, name="wgq", align_bytes=64)
        wgs = keep.tile([P, PASSES, HD], U8, name="wgs", align_bytes=64)
        woq = keep.tile([P, PASSES, DIM], U32, name="woq", align_bytes=64)
        wos = keep.tile([P, PASSES, DIM], U8, name="wos", align_bytes=64)
        bh = keep.tile([P, H], BF16, name="bh")
        bgb = keep.tile([P, PASSES, PACK], BF16, name="bgb")
        bgt = keep.tile([P, PASSES * PACK], F32, name="bgt")
        warm = keep.tile([P, 1], F32, name="warm")
        warm2 = keep.tile([P, 1], F32, name="warm2")

        loads = [("wg", 0, kp) for kp in range(PASSES)] + [("a", 0, 0)]
        for s in range(WEIGHT_STEPS):
            kind, chunk = ("wg", s + 1) if s + 1 < PASSES else ("wo", s + 1 - PASSES)
            loads.extend([(kind, chunk, kp) for kp in range(VECTOR_SHARE)])
            loads.append(("a", s + 1, 0))
            loads.extend([(kind, chunk, kp) for kp in range(VECTOR_SHARE, PASSES)])
        loads.extend([("a", sg, 0) for sg in range(WEIGHT_STEPS + 1, STEPS)])

        raw = {}
        x_raw = {}
        x_sorted = {}
        x_codes = {}
        y_codes = {}
        a_sorted = {}
        head_gates = {}
        state = {"issued": 0, "read": 0, "x_issued": 0, "x_read": 0, "to_quantize": []}

        def fetch():
            first = state["issued"]
            last = min(len(loads), state["read"] + RAW_BUFS)
            for q in range(first, last):
                kind, number, kp = loads[q]
                tile = sb.tile([P, 2048], BF16, name="raw", tag="raw", bufs=RAW_BUFS)
                if kind == "a":
                    blk, grp = divmod(number, PASSES)
                    b, i = divmod(blk, BLOCKS_PER_BATCH)
                    nc.sync.dma_start(
                        out=tile[:].rearrange("p (h e) -> p h e", h=8),
                        in_=a_v[b, i][:, 8 * grp : 8 * grp + 8, :],
                    )
                else:
                    src = wg_v if kind == "wg" else wo_v
                    nc.sync.dma_start(
                        out=tile[:].rearrange("p (j c) -> p j c", j=PACK),
                        in_=src[kp][:, :, WIDE * number : WIDE * (number + 1)],
                    )
                raw[(kind, number, kp)] = tile
            state["issued"] = max(first, last)

        def fetch_x():
            half = state["x_issued"]
            if half < 2 * BLOCKS and half < state["x_read"] + 2:
                blk, side = divmod(half, 2)
                b, i = divmod(blk, BLOCKS_PER_BATCH)
                tile = sb.tile([P, 4, 1024], BF16, name="xr", tag="xr", bufs=2)
                nc.sync.dma_start(out=tile[:], in_=x_v[b, i][:, :, 1024 * side : 1024 * (side + 1)])
                x_raw[half] = tile
                state["x_issued"] = half + 1

        def sort_x(xp):
            if xp < SORTED_FROM or xp >= STEPS:
                return
            half, side = divmod(xp, 2)
            words = x_raw[half][:].rearrange("p j k -> p (j k)").bitcast(F32)
            xo = sb.tile([P, 4, 2, P], F32, name="xo", tag="xo", bufs=2)
            nc.vector.tensor_copy(
                out=xo[:],
                in_=words.rearrange("p (j g w u) -> p j g u w", j=4, g=2, u=2)[:, :, side, :, :],
            )
            x_sorted[xp] = xo
            if side == 1:
                state["x_read"] = half + 1

        def transpose_x(xp):
            if xp >= STEPS:
                return
            half, side = divmod(xp, 2)
            xg = sb.tile([P, 2048], BF16, name="xg", tag="grp", bufs=4, align_bytes=64)
            xgw = xg[:].bitcast(F32).rearrange("p (n u) -> p n u", u=2)
            for jp in range(2):
                bank = ps.tile([P, 2, 2, P], F32, name="xt", tag="tp", bufs=4)
                for jj in range(2):
                    for u in range(2):
                        if xp < SORTED_FROM:
                            words = x_raw[half][:, 2 * jp + jj, :].bitcast(F32)
                            piece = words[:, 256 * side + u : 256 * (side + 1) : 2]
                        else:
                            piece = x_sorted[xp][:, 2 * jp + jj, u, :]
                        nc.tensor.transpose(bank[:, jj, u, :], piece, ident[:])
                nc.scalar.copy(
                    out=xgw[:, 256 * jp : 256 * (jp + 1), :].rearrange(
                        "p (jj r) u -> p jj r u", jj=2
                    ),
                    in_=bank[:].rearrange("p jj u r -> p jj r u"),
                )
            state["to_quantize"].append((xp, xg))
            if xp < SORTED_FROM and side == 1:
                state["x_read"] = half + 1

        def quantize_x():
            for xp, xg in state["to_quantize"]:
                blk, kp = divmod(xp, PASSES)
                if kp == 0:
                    codes = sb.tile([P, PASSES, WIDE], U32, name="xq", tag="xq", bufs=2, align_bytes=64)
                    scales = sb.tile([P, PASSES, WIDE], U8, name="xs", tag="xs", bufs=2, align_bytes=64)
                    x_codes[blk] = (codes, scales)
                codes, scales = x_codes[blk]
                nc.vector.quantize_mx(
                    out=codes[:, kp, :].bitcast(FP8X4), scales=scales[:, kp, :], in_=xg[:]
                )
            state["to_quantize"] = []

        def group_weights(copy, kind, chunk, kp):
            rows = raw[(kind, chunk, kp)]
            grouped = sb.tile([P, 2048], BF16, name="wgp", tag="grp", bufs=4, align_bytes=64)
            if kind == "wg":
                copy(
                    out=grouped[:].rearrange("p (t m j) -> p m j t", t=PACK, j=PACK),
                    in_=rows[:].rearrange("p (j m t) -> p m j t", j=PACK, t=PACK),
                )
            else:
                copy(
                    out=grouped[:].rearrange("p (c i j) -> p c j i", i=4, j=PACK),
                    in_=rows[:].rearrange("p (j c i) -> p c j i", j=PACK, i=4),
                )
            state["read"] = state["read"] + 1
            return grouped

        def quantize_weights(kind, chunk, kp, grouped):
            codes, scales = (wgq, wgs) if kind == "wg" else (woq, wos)
            cols = slice(WIDE * chunk, WIDE * (chunk + 1))
            nc.vector.quantize_mx(
                out=codes[:, kp, cols].bitcast(FP8X4), scales=scales[:, kp, cols], in_=grouped[:]
            )

        def fetch_head_gates(pair):
            if pair >= 2 * BLOCKS:
                return
            blk, side = divmod(pair, 2)
            tile = sb.tile([P, 2, WIDE], F32, name="hgT", tag="hgT", bufs=3)
            for hl in range(8):
                rows = park[blk, 16 * hl + 8 * side : 16 * hl + 8 * side + 8, :]
                nc.sync.dma_start(
                    out=tile[16 * hl : 16 * hl + 16, :, :].rearrange("p g n -> p (g n)"),
                    in_=rows.rearrange("q r -> (q r)").partition_broadcast(16),
                )
            head_gates[pair] = tile

        def sort_a(sg):
            if sg >= STEPS:
                return
            words = raw[("a", sg, 0)][:].bitcast(F32).rearrange(
                "p (h j m u) -> p u j h m", h=8, j=4, u=2
            )
            ao = sb.tile([P, 4, 2, P], F32, name="ao", tag="ao", bufs=2)
            for u in range(2):
                nc.vector.tensor_copy(
                    out=ao[:, :, u, :].rearrange("p j (h m) -> p j h m", h=8), in_=words[:, u]
                )
            a_sorted[sg] = ao
            state["read"] = state["read"] + 1

        def stage1(sg, scalar_share):
            blk, grp = divmod(sg, PASSES)
            codes, scales = x_codes[blk]
            gates = sb.tile([P, PACK, WIDE], F32, name="gt", tag="g", bufs=2)
            for t in range(PACK):
                acc = ps.tile([P, WIDE], F32, name="acc", tag="acc", bufs=4)
                cols = slice(WIDE * grp + P * t, WIDE * grp + P * (t + 1))
                for kp in range(PASSES):
                    nc.tensor.matmul_mx(
                        out=acc[:],
                        lhsT=wgq[:, kp, cols].bitcast(FP8X4),
                        lhsT_scale=wgs[:, kp, cols],
                        rhs=codes[:, kp, :].bitcast(FP8X4),
                        rhs_scale=scales[:, kp, :],
                        start=(kp == 0),
                        stop=(kp == PASSES - 1),
                    )
                nc.scalar.activation(
                    out=gates[:, t, :],
                    in_=acc[:],
                    func=SIGMOID,
                    bias=bgt[:, PACK * grp + t : PACK * grp + t + 1],
                    scale=1.0,
                )
                nc.vector.tensor_tensor(
                    out=gates[:, t, :],
                    in0=gates[:, t, :],
                    in1=head_gates[sg // 2][:, sg % 2, :],
                    op=MULT,
                )
            done = [group_weights(nc.scalar.copy, *piece) for piece in scalar_share]
            return gates, done

        def transpose_a(sg):
            banks = []
            for jp in range(2):
                bank = ps.tile([P, 2, 2, P], F32, name="at", tag="tp", bufs=4)
                for jj in range(2):
                    for u in range(2):
                        nc.tensor.transpose(
                            bank[:, jj, u, :], a_sorted[sg][:, 2 * jp + jj, u, :], ident[:]
                        )
                banks.append(bank)
            return banks

        def multiply_y(gates, banks):
            yg = sb.tile([P, WIDE, PACK], BF16, name="yg", tag="yg", bufs=2, align_bytes=64)
            for j in range(4):
                jp, jj = divmod(j, 2)
                nc.vector.tensor_tensor(
                    out=yg[:, P * j : P * (j + 1), :].rearrange("p r (u e) -> p r u e", e=2),
                    in0=banks[jp][:, jj, :, :].bitcast(BF16).rearrange("p u (r e) -> p r u e", e=2),
                    in1=gates[:, :, P * j : P * (j + 1)].rearrange("p (u e) r -> p r u e", e=2),
                    op=MULT,
                )
            return yg

        def quantize_y(sg, yg):
            blk, grp = divmod(sg, PASSES)
            if grp == 0:
                codes = sb.tile([P, PASSES, WIDE], U32, name="yq", tag="yq", bufs=2, align_bytes=64)
                scales = sb.tile([P, PASSES, WIDE], U8, name="ys", tag="ys", bufs=2, align_bytes=64)
                y_codes[blk] = (codes, scales)
            codes, scales = y_codes[blk]
            nc.vector.quantize_mx(
                out=codes[:, grp, :].bitcast(FP8X4),
                scales=scales[:, grp, :],
                in_=yg[:].rearrange("p n t -> p (n t)"),
            )

        def stage2(og):
            blk, colgrp = divmod(og, PASSES)
            b, i = divmod(blk, BLOCKS_PER_BATCH)
            codes, scales = y_codes[blk]
            cols = slice(WIDE * colgrp, WIDE * (colgrp + 1))
            for j in range(4):
                acc = ps.tile([P, WIDE], F32, name="acc", tag="acc", bufs=4)
                toks = slice(P * j, P * (j + 1))
                for kp in range(PASSES):
                    nc.tensor.matmul_mx(
                        out=acc[:],
                        lhsT=codes[:, kp, toks].bitcast(FP8X4),
                        lhsT_scale=scales[:, kp, toks],
                        rhs=woq[:, kp, cols].bitcast(FP8X4),
                        rhs_scale=wos[:, kp, cols],
                        start=(kp == 0),
                        stop=(kp == PASSES - 1),
                    )
                ot = sb.tile([P, WIDE], F32, name="ot", tag="o", bufs=4)
                nc.scalar.copy(out=ot[:], in_=acc[:])
                nc.sync.dma_start(out=out_v[b, i, j][:, cols], in_=ot[:])

        hl = sb.tile([P, BLOCKS, 4 * H], BF16, name="hl", tag="xo", bufs=2)
        nc.scalar.dma_start(out=hl[:], in_=hg_v)
        nc.scalar.dma_start(out=bh[:], in_=bhg.partition_broadcast(P))
        nc.scalar.dma_start(out=bgb[:], in_=bg_v)
        fetch_x()
        fetch_x()
        fetch()
        make_identity(nc, ident[:])
        nc.vector.memset(warm[:], 0.0)
        nc.scalar.activation(out=warm2[:], in_=warm[:], func=SIGMOID)
        nc.vector.tensor_copy(out=bgt[:], in_=bgb[:].rearrange("p g t -> p (g t)"))

        hgs = sb.tile([P, BLOCKS, 4, H], F32, name="hgs", tag="g", bufs=2)
        nc.vector.tensor_tensor(
            out=hgs[:].rearrange("p a j h -> p (a j) h"),
            in0=hl[:].rearrange("p a (j h) -> p (a j) h", j=4),
            in1=bh[:].unsqueeze(1).to_broadcast([P, 4 * BLOCKS, H]),
            op=ADD,
        )
        nc.scalar.activation(out=hgs[:], in_=hgs[:], func=SIGMOID)
        hgp = sb.tile([P, BLOCKS, P], F32, name="hgp", tag="g", bufs=2)
        for blk in range(BLOCKS):
            nc.vector.tensor_copy(
                out=hgp[:, blk, :].rearrange("p (h g j) -> p h g j", h=8, g=PASSES),
                in_=hgs[:, blk, :, :].rearrange("p j (g h) -> p h g j", g=PASSES),
            )
        hT = sb.tile([P, BLOCKS, P], F32, name="hT", tag="yq", bufs=2, align_bytes=64)
        for first in range(0, BLOCKS, 4):
            bank = ps.tile([P, 4, P], F32, name="ht", tag="tp", bufs=4)
            for q in range(4):
                nc.tensor.transpose(bank[:, q, :], hgp[:, first + q, :], ident[:])
            nc.scalar.copy(out=hT[:, first : first + 4, :], in_=bank[:])
            nc.scalar.dma_start(
                out=park[first : first + 4].rearrange("k q r -> q k r"),
                in_=hT[:, first : first + 4, :],
            )

        transpose_x(0)
        transpose_x(1)
        w0 = group_weights(nc.vector.tensor_copy, "wg", 0, 0)
        quantize_x()
        transpose_x(2)
        transpose_x(3)
        w1 = group_weights(nc.vector.tensor_copy, "wg", 0, 1)
        quantize_x()
        quantize_weights("wg", 0, 0, w0)
        w2 = group_weights(nc.vector.tensor_copy, "wg", 0, 2)
        w3 = group_weights(nc.scalar.copy, "wg", 0, 3)
        quantize_weights("wg", 0, 1, w1)
        quantize_weights("wg", 0, 2, w2)
        quantize_weights("wg", 0, 3, w3)
        fetch()
        fetch_head_gates(0)
        sort_a(0)
        fetch_x()

        for s in range(STEPS + LAG):
            fetch()
            fetch_x()
            quantize_x()
            if s % 2 == 0:
                fetch_head_gates(s // 2 + 1)
            sort_x(s + X_AHEAD + 1)
            vector_share = []
            scalar_share = []
            if s < WEIGHT_STEPS:
                kind, chunk = ("wg", s + 1) if s + 1 < PASSES else ("wo", s + 1 - PASSES)
                vector_share = [
                    group_weights(nc.vector.tensor_copy, kind, chunk, kp)
                    for kp in range(VECTOR_SHARE)
                ]
                scalar_share = [(kind, chunk, kp) for kp in range(VECTOR_SHARE, PASSES)]
            sort_a(s + 1)
            for kp in range(len(vector_share)):
                quantize_weights(kind, chunk, kp, vector_share[kp])
            fetch()
            if s < STEPS:
                gates, done = stage1(s, scalar_share)
                fetch()
                for q in range(len(done)):
                    quantize_weights(kind, chunk, VECTOR_SHARE + q, done[q])
                if s == 0:
                    transpose_x(X_AHEAD - 1)
                transpose_x(s + X_AHEAD)
                banks = transpose_a(s)
                yg = multiply_y(gates, banks)
            if s >= LAG:
                stage2(s - LAG)
            if s < STEPS:
                quantize_y(s, yg)
